import numpy as np
import ml_dtypes


def mxq(x, axis, fmt="e4m3"):
    dtype, down = {"e4m3": (ml_dtypes.float8_e4m3fn, 7), "e5m2": (ml_dtypes.float8_e5m2, 14)}[fmt]
    v = np.moveaxis(np.asarray(x, np.float32).astype(ml_dtypes.bfloat16).astype(np.float64), axis, -1)
    blocks = v.reshape(v.shape[:-1] + (-1, 32))
    amax = np.abs(blocks).max(-1, keepdims=True)
    byte = np.maximum(np.where(amax > 0, np.frexp(amax)[1] - 1 + 127, 0) - down, 1)
    scale = np.exp2(byte - 127.0)
    codes = (blocks / scale).astype(np.float32).astype(dtype).astype(np.float64)
    return np.moveaxis((codes * scale).reshape(v.shape), -1, axis)


WIDE = False


def mx_kscale(k):
    if not WIDE:
        return np.ones(k)
    levels = np.array([10, -10, 5, -5, 0])
    if k % 512:
        return np.exp2(np.random.permutation(np.resize(levels, k // 32))).repeat(32)
    a = np.empty((k // 512, 16))
    for p in range(k // 512):
        a[p, :8] = np.random.permutation(np.resize(levels, 8))
        for g in range(8):
            far = levels[np.abs(levels - a[p, g]) >= 10]
            a[p, g + 8] = far[np.random.randint(len(far))]
    return np.exp2(a.ravel()).repeat(32)


BF16 = ml_dtypes.bfloat16


def bf(x):
    return np.asarray(x, np.float32).astype(BF16)


def f64(x):
    return np.asarray(x).astype(np.float64)


B, T, C, H, S, L, QB = 1, 1024, 1024, 8, 512, 1024, 512
HD = C // H
N = S + T
THETA = 10000.0


def rope_cos_sin():
    inv = 1.0 / (THETA ** (np.arange(0, HD, 2) / HD))
    ang = np.outer(np.arange(N), inv)
    return np.cos(ang), np.sin(ang)


def apply_rope(u, cos, sin):
    ur = u.reshape(B, N, H, HD // 2, 2)
    u0, u1 = ur[..., 0], ur[..., 1]
    c = cos[None, :, None, :]
    s = sin[None, :, None, :]
    return np.stack([u0 * c - u1 * s, u0 * s + u1 * c], axis=-1).reshape(B, N, H, HD)


def setup_inputs():
    s = mx_kscale(C)
    col = np.concatenate([np.full(2 * C, 0.9), np.full(C, 4.0)]) / np.sqrt(C)
    return {"x": bf(np.random.standard_normal((B, T, C)) * s),
            "short_term_memory": bf(np.random.standard_normal((B, S, C)) * s),
            "w_attn": bf(np.random.standard_normal((C, 3 * C)) * col / s[:, None])}


def reference(x, short_term_memory, w_attn):
    xcat = np.concatenate([f64(short_term_memory), f64(x)], axis=1)
    qkv = mxq(xcat, 2, "e4m3") @ mxq(f64(w_attn), 0, "e4m3")
    q, k, v = np.split(qkv, 3, axis=-1)
    q = q.reshape(B, N, H, HD)
    k = k.reshape(B, N, H, HD)
    v = v.reshape(B, N, H, HD)
    cos, sin = rope_cos_sin()
    return apply_rope(q, cos, sin), apply_rope(k, cos, sin), v

@@ -1,0 +1,265 @@
+import math
+from contextlib import ExitStack
+
+import concourse.mybir as mybir
+from concourse.masks import make_identity
+
+F32 = mybir.dt.float32
+BF16 = mybir.dt.bfloat16
+I32 = mybir.dt.int32
+U32 = mybir.dt.uint32
+U8 = mybir.dt.uint8
+FP8X4 = mybir.dt.float8_e4m3fn_x4
+ALU = mybir.AluOpType
+ACT = mybir.ActivationFunctionType
+
+P = 128
+PACK = 4
+K_PASS = P * PACK
+MEMORY_TOKENS = 512
+TOKENS = 1536
+C = 1024
+PASSES = C // K_PASS
+TILES = TOKENS // P
+MEMORY_TILES = MEMORY_TOKENS // P
+BANK = 512
+HALVES = C // BANK
+HEAD = 128
+PAIRS = HEAD // 2
+BANK_HEADS = BANK // HEAD
+THETA = 10000.0
+Q, K, V = 0, 1, 2
+ROUND_MAGIC = 1.5 * 2.0**23
+
+FLOPS = 2 * TOKENS * C * 3 * C
+
+
+def tile_memoryselfattention_pa_kernel(tc, x, short_term_memory, w_attn, out_0, out_1, out_2):
+    nc = tc.nc
+    memory_rows = short_term_memory.flatten_outer_dims()
+    x_rows = x.flatten_outer_dims()
+    outs = [o.rearrange("b n h d -> (b n) (h d)") for o in (out_0, out_1, out_2)]
+
+    with ExitStack() as ctx:
+        keep = ctx.enter_context(tc.tile_pool(name="keep", bufs=1))
+        x_stage = ctx.enter_context(tc.tile_pool(name="x_stage", bufs=2))
+        w_stage = ctx.enter_context(tc.tile_pool(name="w_stage", bufs=4))
+        products = ctx.enter_context(tc.tile_pool(name="products", bufs=3))
+        rope_results = ctx.enter_context(tc.tile_pool(name="rope_results", bufs=4))
+        plain_results = ctx.enter_context(tc.tile_pool(name="plain_results", bufs=3))
+        psum_x = ctx.enter_context(tc.psum_pool(name="psum_x", bufs=2))
+        psum_rope = ctx.enter_context(tc.psum_pool(name="psum_rope", bufs=4))
+        psum_plain = ctx.enter_context(tc.psum_pool(name="psum_plain", bufs=2))
+        ctx.enter_context(tc.manual_schedule())
+
+        x_raw = keep.tile([P, TILES, C], BF16)
+        w_raw = keep.tile([P, 3, PASSES * PACK, C], BF16)
+
+        def load_x(m):
+            if m < MEMORY_TILES:
+                rows = memory_rows[m * P : (m + 1) * P, :]
+            else:
+                rows = x_rows[(m - MEMORY_TILES) * P : (m - MEMORY_TILES + 1) * P, :]
+            nc.sync.dma_start(out=x_raw[:, m, :], in_=rows)
+
+        def load_w(third):
+            for g in range(PASSES):
+                nc.sync.dma_start(
+                    out=w_raw[:, third, PACK * g : PACK * (g + 1), :],
+                    in_=w_attn[K_PASS * g : K_PASS * (g + 1), third * C : (third + 1) * C].rearrange(
+                        "(p t) c -> p t c", t=PACK
+                    ),
+                )
+
+        load_x(0)
+        load_x(1)
+        load_w(Q)
+        for m in range(2, TILES):
+            load_x(m)
+        load_w(V)
+        load_w(K)
+
+        warm = keep.tile([P, 1], F32)
+        nc.vector.memset(warm[:], 0.0)
+        warm_out = keep.tile([P, 1], F32)
+        nc.scalar.activation(out=warm_out[:], in_=warm[:], func=ACT.Sin)
+
+        position_int = keep.tile([P, TILES], I32)
+        nc.gpsimd.iota(position_int[:], pattern=[[P, TILES]], base=0, channel_multiplier=1)
+        identity = keep.tile([P, P], F32)
+        make_identity(nc, identity[:])
+        position = keep.tile([P, TILES], F32)
+        nc.vector.tensor_copy(out=position[:], in_=position_int[:])
+
+        one = keep.tile([P, 1], F32)
+        nc.vector.memset(one[:], 1.0)
+        turns_per_step = keep.tile([P, PAIRS], F32)
+        nc.vector.tensor_scalar_mul(out=turns_per_step[:, 0:1], in0=one[:], scalar1=1.0 / (2.0 * math.pi))
+        width = 1
+        while width < PAIRS:
+            nc.vector.tensor_scalar_mul(
+                out=turns_per_step[:, width : 2 * width],
+                in0=turns_per_step[:, 0:width],
+                scalar1=THETA ** (-width / PAIRS),
+            )
+            width *= 2
+
+        turns = keep.tile([P, 2, TILES, PAIRS], F32)
+        nc.vector.tensor_tensor(
+            out=turns[:, 0, :, :],
+            in0=position[:].unsqueeze(2).to_broadcast([P, TILES, PAIRS]),
+            in1=turns_per_step[:].unsqueeze(1).to_broadcast([P, TILES, PAIRS]),
+            op=ALU.mult,
+        )
+        nc.vector.tensor_scalar_add(out=turns[:, 1, :, :], in0=turns[:, 0, :, :], scalar1=-0.25)
+        nearest = keep.tile([P, 2, TILES, PAIRS], F32)
+        nc.vector.tensor_scalar_add(out=nearest[:], in0=turns[:], scalar1=ROUND_MAGIC)
+        nc.vector.scalar_tensor_tensor(
+            out=nearest[:], in0=nearest[:], scalar=ROUND_MAGIC, in1=turns[:], op0=ALU.subtract, op1=ALU.subtract
+        )
+        distance = keep.tile([P, 3, TILES, PAIRS], F32)
+        nc.vector.scalar_tensor_tensor(
+            out=distance[:, 1:3, :, :], in0=nearest[:], scalar=-1.0, in1=nearest[:], op0=ALU.mult, op1=ALU.max
+        )
+        nc.vector.tensor_scalar(
+            out=distance[:, 0, :, :], in0=distance[:, 2, :, :], scalar1=-1.0, scalar2=0.5, op0=ALU.mult, op1=ALU.add
+        )
+        rope = keep.tile([P, TILES, 2, PAIRS, 2], F32)
+
+        def take_sines():
+            for member in range(2):
+                nc.scalar.activation(
+                    out=rope[:, :, member, :, :],
+                    in_=distance[:, 1 - member : 3 - member, :, :].rearrange("p z m i -> p m i z"),
+                    func=ACT.Sin,
+                    scale=-2.0 * math.pi,
+                    bias=math.pi / 2.0,
+                )
+
+        x_codes = keep.tile([P, TILES * PASSES * P], U32, align_bytes=64)
+        x_scales = keep.tile([P, TILES * PASSES * P], U8, align_bytes=64)
+        TILE_WORDS = PASSES * P
+
+        x_grouped = {}
+
+        def transpose_x_pair(pair):
+            grouped = x_stage.tile([P, 2 * TILE_WORDS * PACK], BF16, align_bytes=64, name="x_grouped")
+            x_grouped[pair] = grouped
+            grouped_words = grouped[:].bitcast(F32).rearrange("p (a g r u) -> p a g r u", a=2, g=PASSES, u=2)
+            for a in range(2):
+                m = 2 * pair + a
+                x_words = x_raw[:, m, :].bitcast(F32)
+                flipped = psum_x.tile([P, PASSES * 2, P], F32)
+                for j in range(PASSES * 2):
+                    first = (j // 2) * 2 * P + j % 2
+                    nc.tensor.transpose(flipped[:, j, :], x_words[:, first : first + 2 * P - 1 : 2], identity[:])
+                nc.scalar.copy(
+                    out=grouped_words[:, a], in_=flipped[:].rearrange("p (g u) r -> p g r u", g=PASSES)
+                )
+
+        def quantise_x_pair(pair):
+            words = slice(2 * pair * TILE_WORDS, 2 * (pair + 1) * TILE_WORDS)
+            nc.vector.quantize_mx(
+                out=x_codes[:, words].bitcast(FP8X4), scales=x_scales[:, words], in_=x_grouped[pair][:]
+            )
+
+        w_codes = keep.tile([P, 3 * PASSES * C], U32, align_bytes=64)
+        w_scales = keep.tile([P, 3 * PASSES * C], U8, align_bytes=64)
+        w_grouped = {}
+
+        def w_words(third, g, half):
+            start = (third * PASSES + g) * C + half * BANK
+            return slice(start, start + BANK)
+
+        def regroup_w(piece, on_vector):
+            third, g, half = piece
+            grouped = w_stage.tile([P, BANK, PACK], BF16, align_bytes=64, name="w_grouped")
+            w_grouped[piece] = grouped
+            rows = w_raw[:, third, g * PACK : (g + 1) * PACK, half * BANK : (half + 1) * BANK]
+            dst = grouped[:].rearrange("p (c i) t -> p c t i", i=4)
+            src = rows.rearrange("p t (c i) -> p c t i", i=4)
+            if on_vector:
+                nc.vector.tensor_copy(out=dst, in_=src)
+            else:
+                nc.scalar.copy(out=dst, in_=src)
+
+        def quantise_w(piece):
+            words = w_words(*piece)
+            nc.vector.quantize_mx(
+                out=w_codes[:, words].bitcast(FP8X4),
+                scales=w_scales[:, words],
+                in_=w_grouped[piece][:].rearrange("p c t -> p (c t)"),
+            )
+
+        def pieces_of(third):
+            return [(third, g, half) for g in range(PASSES) for half in range(HALVES)]
+
+        def project(pool, third, m, half):
+            acc = pool.tile([P, BANK], F32, name="acc")
+            for g in range(PASSES):
+                tokens = slice(m * TILE_WORDS + g * P, m * TILE_WORDS + (g + 1) * P)
+                words = w_words(third, g, half)
+                nc.tensor.matmul_mx(
+                    out=acc[:],
+                    lhsT=x_codes[:, tokens].bitcast(FP8X4),
+                    lhsT_scale=x_scales[:, tokens],
+                    rhs=w_codes[:, words].bitcast(FP8X4),
+                    rhs_scale=w_scales[:, words],
+                    start=(g == 0),
+                    stop=(g == PASSES - 1),
+                )
+            return acc
+
+        def store(third, m, result):
+            nc.sync.dma_start(out=outs[third][m * P : (m + 1) * P, :], in_=result[:])
+
+        def rope_step(third, m):
+            shape = [P, 2, BANK_HEADS, PAIRS, 2]
+            product = products.tile([P, 2, C], F32, name="product")
+            for half in range(HALVES):
+                acc = project(psum_rope, third, m, half)
+                nc.vector.tensor_tensor(
+                    out=product[:, :, half * BANK : (half + 1) * BANK].rearrange(
+                        "p x (h i z) -> p x h i z", h=BANK_HEADS, z=2
+                    ),
+                    in0=acc[:].rearrange("p (h i x) -> p x h i", h=BANK_HEADS, x=2).unsqueeze(4).to_broadcast(shape),
+                    in1=rope[:, m, :, :, :].unsqueeze(2).to_broadcast(shape),
+                    op=ALU.mult,
+                )
+            result = rope_results.tile([P, C], F32, name="rope_result")
+            nc.gpsimd.tensor_tensor(out=result[:], in0=product[:, 0, :], in1=product[:, 1, :], op=ALU.add)
+            store(third, m, result)
+
+        def plain_step(third, m):
+            result = plain_results.tile([P, C], F32, name="plain_result")
+            for half in range(HALVES):
+                acc = project(psum_plain, third, m, half)
+                nc.scalar.copy(out=result[:, half * BANK : (half + 1) * BANK], in_=acc[:])
+            store(third, m, result)
+
+        X_PAIRS = TILES // 2
+        transpose_x_pair(0)
+        quantise_x_pair(0)
+        for piece in pieces_of(Q):
+            regroup_w(piece, on_vector=(piece[2] == 0))
+        take_sines()
+        for piece in pieces_of(Q):
+            quantise_w(piece)
+
+        later_pieces = pieces_of(V) + pieces_of(K)
+        rope_steps = [(third, m) for third in (Q, K) for m in range(TILES)]
+        FIRST_PIECE_STEP = 3
+        assert FIRST_PIECE_STEP + len(later_pieces) < TILES
+        FIRST_PLAIN_STEP = FIRST_PIECE_STEP + len(pieces_of(V)) + 1
+        for step, (third, m) in enumerate(rope_steps):
+            if 1 <= step < X_PAIRS:
+                quantise_x_pair(step)
+            rope_step(third, m)
+            if step + 1 < X_PAIRS:
+                transpose_x_pair(step + 1)
+            if 0 <= step - FIRST_PIECE_STEP < len(later_pieces):
+                regroup_w(later_pieces[step - FIRST_PIECE_STEP], on_vector=False)
+            if 0 <= step - FIRST_PIECE_STEP - 1 < len(later_pieces):
+                quantise_w(later_pieces[step - FIRST_PIECE_STEP - 1])
+            if 0 <= step - FIRST_PLAIN_STEP < TILES:
+                plain_step(V, step - FIRST_PLAIN_STEP)

@@ -32,6 +32,7 @@ Q, K, V = 0, 1, 2
 ROUND_MAGIC = 1.5 * 2.0**23
 
 FLOPS = 2 * TOKENS * C * 3 * C
+TWO_PI = 2.0 * math.pi
 
 
 def tile_memoryselfattention_pa_kernel(tc, x, short_term_memory, w_attn, out_0, out_1, out_2):
@@ -42,10 +43,10 @@ def tile_memoryselfattention_pa_kernel(tc, x, short_term_memory, w_attn, out_0, 
 
     with ExitStack() as ctx:
         keep = ctx.enter_context(tc.tile_pool(name="keep", bufs=1))
-        x_stage = ctx.enter_context(tc.tile_pool(name="x_stage", bufs=2))
+        w_load = ctx.enter_context(tc.tile_pool(name="w_load", bufs=4))
         w_stage = ctx.enter_context(tc.tile_pool(name="w_stage", bufs=4))
-        products = ctx.enter_context(tc.tile_pool(name="products", bufs=3))
-        rope_results = ctx.enter_context(tc.tile_pool(name="rope_results", bufs=4))
+        products = ctx.enter_context(tc.tile_pool(name="products", bufs=4))
+        rope_results = ctx.enter_context(tc.tile_pool(name="rope_results", bufs=6))
         plain_results = ctx.enter_context(tc.tile_pool(name="plain_results", bufs=3))
         psum_x = ctx.enter_context(tc.psum_pool(name="psum_x", bufs=2))
         psum_rope = ctx.enter_context(tc.psum_pool(name="psum_rope", bufs=4))
@@ -53,31 +54,35 @@ def tile_memoryselfattention_pa_kernel(tc, x, short_term_memory, w_attn, out_0, 
         ctx.enter_context(tc.manual_schedule())
 
         x_raw = keep.tile([P, TILES, C], BF16)
-        w_raw = keep.tile([P, 3, PASSES * PACK, C], BF16)
+        w_raw = {}
 
-        def load_x(m):
-            if m < MEMORY_TILES:
-                rows = memory_rows[m * P : (m + 1) * P, :]
+        def load_x(first, count):
+            if first < MEMORY_TILES:
+                rows = memory_rows[first * P : (first + count) * P, :]
             else:
-                rows = x_rows[(m - MEMORY_TILES) * P : (m - MEMORY_TILES + 1) * P, :]
-            nc.sync.dma_start(out=x_raw[:, m, :], in_=rows)
+                rows = x_rows[(first - MEMORY_TILES) * P : (first - MEMORY_TILES + count) * P, :]
+            nc.sync.dma_start(
+                out=x_raw[:, first : first + count, :], in_=rows.rearrange("(m p) c -> p m c", p=P)
+            )
 
-        def load_w(third):
-            for g in range(PASSES):
-                nc.sync.dma_start(
-                    out=w_raw[:, third, PACK * g : PACK * (g + 1), :],
-                    in_=w_attn[K_PASS * g : K_PASS * (g + 1), third * C : (third + 1) * C].rearrange(
-                        "(p t) c -> p t c", t=PACK
-                    ),
-                )
+        def load_w(third, g, first, width):
+            if (third, g) not in w_raw:
+                w_raw[third, g] = w_load.tile([P, PACK, C], BF16, name="w_raw")
+            columns = slice(third * C + first, third * C + first + width)
+            nc.sync.dma_start(
+                out=w_raw[third, g][:, :, first : first + width],
+                in_=w_attn[K_PASS * g : K_PASS * (g + 1), columns].rearrange("(p t) c -> p t c", t=PACK),
+            )
 
-        load_x(0)
-        load_x(1)
-        load_w(Q)
-        for m in range(2, TILES):
-            load_x(m)
-        load_w(V)
-        load_w(K)
+        load_x(0, 1)
+        load_w(Q, 0, 0, BANK)
+        load_w(Q, 1, 0, BANK)
+        load_x(1, 1)
+        load_x(2, 2)
+        load_w(Q, 0, BANK, BANK)
+        load_w(Q, 1, BANK, BANK)
+        load_x(4, 4)
+        load_x(8, 4)
 
         warm = keep.tile([P, 1], F32)
         nc.vector.memset(warm[:], 0.0)
@@ -88,13 +93,13 @@ def tile_memoryselfattention_pa_kernel(tc, x, short_term_memory, w_attn, out_0, 
         nc.gpsimd.iota(position_int[:], pattern=[[P, TILES]], base=0, channel_multiplier=1)
         identity = keep.tile([P, P], F32)
         make_identity(nc, identity[:])
-        position = keep.tile([P, TILES], F32)
-        nc.vector.tensor_copy(out=position[:], in_=position_int[:])
 
         one = keep.tile([P, 1], F32)
         nc.vector.memset(one[:], 1.0)
         turns_per_step = keep.tile([P, PAIRS], F32)
-        nc.vector.tensor_scalar_mul(out=turns_per_step[:, 0:1], in0=one[:], scalar1=1.0 / (2.0 * math.pi))
+        nc.vector.tensor_scalar_mul(out=turns_per_step[:, 0:1], in0=one[:], scalar1=1.0 / TWO_PI)
+        position = keep.tile([P, TILES], F32)
+        nc.vector.tensor_copy(out=position[:], in_=position_int[:])
         width = 1
         while width < PAIRS:
             nc.vector.tensor_scalar_mul(
@@ -104,63 +109,68 @@ def tile_memoryselfattention_pa_kernel(tc, x, short_term_memory, w_attn, out_0, 
             )
             width *= 2
 
-        turns = keep.tile([P, 2, TILES, PAIRS], F32)
+        phase = keep.tile([P, 3, TILES, PAIRS], F32)
+        turns = keep.tile([P, TILES, PAIRS], F32)
         nc.vector.tensor_tensor(
-            out=turns[:, 0, :, :],
+            out=turns[:],
             in0=position[:].unsqueeze(2).to_broadcast([P, TILES, PAIRS]),
             in1=turns_per_step[:].unsqueeze(1).to_broadcast([P, TILES, PAIRS]),
             op=ALU.mult,
         )
-        nc.vector.tensor_scalar_add(out=turns[:, 1, :, :], in0=turns[:, 0, :, :], scalar1=-0.25)
-        nearest = keep.tile([P, 2, TILES, PAIRS], F32)
-        nc.vector.tensor_scalar_add(out=nearest[:], in0=turns[:], scalar1=ROUND_MAGIC)
+        scratch = keep.tile([P, TILES, PAIRS], F32)
+        nc.vector.tensor_scalar_add(out=scratch[:], in0=turns[:], scalar1=ROUND_MAGIC)
         nc.vector.scalar_tensor_tensor(
-            out=nearest[:], in0=nearest[:], scalar=ROUND_MAGIC, in1=turns[:], op0=ALU.subtract, op1=ALU.subtract
+            out=phase[:, 0, :, :], in0=scratch[:], scalar=ROUND_MAGIC, in1=turns[:], op0=ALU.subtract, op1=ALU.subtract
         )
-        distance = keep.tile([P, 3, TILES, PAIRS], F32)
+
+
         nc.vector.scalar_tensor_tensor(
-            out=distance[:, 1:3, :, :], in0=nearest[:], scalar=-1.0, in1=nearest[:], op0=ALU.mult, op1=ALU.max
+            out=scratch[:], in0=phase[:, 0, :, :], scalar=-1.0, in1=phase[:, 0, :, :], op0=ALU.mult, op1=ALU.max
         )
-        nc.vector.tensor_scalar(
-            out=distance[:, 0, :, :], in0=distance[:, 2, :, :], scalar1=-1.0, scalar2=0.5, op0=ALU.mult, op1=ALU.add
-        )
+
+        def finish_phase(first, last):
+            some = slice(first, last)
+            nc.gpsimd.tensor_scalar(
+                out=phase[:, 2, some, :], in0=phase[:, 0, some, :], scalar1=-1.0, scalar2=0.0, op0=ALU.mult, op1=ALU.add
+            )
+            nc.gpsimd.tensor_scalar(
+                out=phase[:, 1, some, :], in0=scratch[:, some, :], scalar1=-1.0, scalar2=0.25, op0=ALU.mult, op1=ALU.add
+            )
+
         rope = keep.tile([P, TILES, 2, PAIRS, 2], F32)
 
-        def take_sines():
+        def take_sines(first, last):
             for member in range(2):
                 nc.scalar.activation(
-                    out=rope[:, :, member, :, :],
-                    in_=distance[:, 1 - member : 3 - member, :, :].rearrange("p z m i -> p m i z"),
+                    out=rope[:, first:last, member, :, :],
+                    in_=phase[:, member : member + 2, first:last, :].rearrange("p z m i -> p m i z"),
                     func=ACT.Sin,
-                    scale=-2.0 * math.pi,
-                    bias=math.pi / 2.0,
+                    scale=TWO_PI,
                 )
 
-        x_codes = keep.tile([P, TILES * PASSES * P], U32, align_bytes=64)
-        x_scales = keep.tile([P, TILES * PASSES * P], U8, align_bytes=64)
         TILE_WORDS = PASSES * P
+        x_grouped = keep.tile([P, TILES * TILE_WORDS * PACK], BF16, align_bytes=64)
+        x_codes = keep.tile([P, TILES * TILE_WORDS], U32, align_bytes=64)
+        x_scales = keep.tile([P, TILES * TILE_WORDS], U8, align_bytes=64)
 
-        x_grouped = {}
+        def transpose_x(m):
+            x_words = x_raw[:, m, :].bitcast(F32)
+            flipped = psum_x.tile([P, PASSES * 2, P], F32, name="flipped")
+            for j in range(PASSES * 2):
+                first = (j // 2) * 2 * P + j % 2
+                nc.tensor.transpose(flipped[:, j, :], x_words[:, first : first + 2 * P - 1 : 2], identity[:])
+            values = slice(m * TILE_WORDS * PACK, (m + 1) * TILE_WORDS * PACK)
+            nc.scalar.copy(
+                out=x_grouped[:, values].bitcast(F32).rearrange("p (g r u) -> p g r u", g=PASSES, u=2),
+                in_=flipped[:].rearrange("p (g u) r -> p g r u", g=PASSES),
+            )
 
-        def transpose_x_pair(pair):
-            grouped = x_stage.tile([P, 2 * TILE_WORDS * PACK], BF16, align_bytes=64, name="x_grouped")
-            x_grouped[pair] = grouped
-            grouped_words = grouped[:].bitcast(F32).rearrange("p (a g r u) -> p a g r u", a=2, g=PASSES, u=2)
-            for a in range(2):
-                m = 2 * pair + a
-                x_words = x_raw[:, m, :].bitcast(F32)
-                flipped = psum_x.tile([P, PASSES * 2, P], F32)
-                for j in range(PASSES * 2):
-                    first = (j // 2) * 2 * P + j % 2
-                    nc.tensor.transpose(flipped[:, j, :], x_words[:, first : first + 2 * P - 1 : 2], identity[:])
-                nc.scalar.copy(
-                    out=grouped_words[:, a], in_=flipped[:].rearrange("p (g u) r -> p g r u", g=PASSES)
-                )
-
-        def quantise_x_pair(pair):
-            words = slice(2 * pair * TILE_WORDS, 2 * (pair + 1) * TILE_WORDS)
+        def quantise_x(first, last):
+            words = slice(first * TILE_WORDS, last * TILE_WORDS)
             nc.vector.quantize_mx(
-                out=x_codes[:, words].bitcast(FP8X4), scales=x_scales[:, words], in_=x_grouped[pair][:]
+                out=x_codes[:, words].bitcast(FP8X4),
+                scales=x_scales[:, words],
+                in_=x_grouped[:, first * TILE_WORDS * PACK : last * TILE_WORDS * PACK],
             )
 
         w_codes = keep.tile([P, 3 * PASSES * C], U32, align_bytes=64)
@@ -171,17 +181,22 @@ def tile_memoryselfattention_pa_kernel(tc, x, short_term_memory, w_attn, out_0, 
             start = (third * PASSES + g) * C + half * BANK
             return slice(start, start + BANK)
 
-        def regroup_w(piece, on_vector):
+        def regroup_w(piece, engine_copy):
             third, g, half = piece
             grouped = w_stage.tile([P, BANK, PACK], BF16, align_bytes=64, name="w_grouped")
             w_grouped[piece] = grouped
-            rows = w_raw[:, third, g * PACK : (g + 1) * PACK, half * BANK : (half + 1) * BANK]
-            dst = grouped[:].rearrange("p (c i) t -> p c t i", i=4)
-            src = rows.rearrange("p t (c i) -> p c t i", i=4)
-            if on_vector:
-                nc.vector.tensor_copy(out=dst, in_=src)
+            rows = w_raw[third, g][:, :, half * BANK : (half + 1) * BANK]
+            if third == V:
+                engine_copy(
+                    out=grouped[:].rearrange("p (c i) t -> p c t i", i=4),
+                    in_=rows.rearrange("p t (c i) -> p c t i", i=4),
+                )
             else:
-                nc.scalar.copy(out=dst, in_=src)
+                for x in range(2):
+                    engine_copy(
+                        out=grouped[:, x * BANK // 2 : (x + 1) * BANK // 2, :].rearrange("p (c i) t -> p c t i", i=4),
+                        in_=rows.rearrange("p t (c i x) -> p x c t i", i=4, x=2)[:, 1 - x],
+                    )
 
         def quantise_w(piece):
             words = w_words(*piece)
@@ -191,75 +206,127 @@ def tile_memoryselfattention_pa_kernel(tc, x, short_term_memory, w_attn, out_0, 
                 in_=w_grouped[piece][:].rearrange("p c t -> p (c t)"),
             )
 
-        def pieces_of(third):
-            return [(third, g, half) for g in range(PASSES) for half in range(HALVES)]
+        def multiply_mx(acc, m, g, words, start, stop):
+            tokens = slice(m * TILE_WORDS + g * P, m * TILE_WORDS + (g + 1) * P)
+            nc.tensor.matmul_mx(
+                out=acc,
+                lhsT=x_codes[:, tokens].bitcast(FP8X4),
+                lhsT_scale=x_scales[:, tokens],
+                rhs=w_codes[:, words].bitcast(FP8X4),
+                rhs_scale=w_scales[:, words],
+                start=start,
+                stop=stop,
+            )
 
         def project(pool, third, m, half):
             acc = pool.tile([P, BANK], F32, name="acc")
             for g in range(PASSES):
-                tokens = slice(m * TILE_WORDS + g * P, m * TILE_WORDS + (g + 1) * P)
-                words = w_words(third, g, half)
-                nc.tensor.matmul_mx(
-                    out=acc[:],
-                    lhsT=x_codes[:, tokens].bitcast(FP8X4),
-                    lhsT_scale=x_scales[:, tokens],
-                    rhs=w_codes[:, words].bitcast(FP8X4),
-                    rhs_scale=w_scales[:, words],
-                    start=(g == 0),
-                    stop=(g == PASSES - 1),
-                )
+                multiply_mx(acc[:], m, g, w_words(third, g, half), g == 0, g == PASSES - 1)
             return acc
 
-        def store(third, m, result):
-            nc.sync.dma_start(out=outs[third][m * P : (m + 1) * P, :], in_=result[:])
+        def store(third, m, first, width, result):
+            nc.sync.dma_start(out=outs[third][m * P : (m + 1) * P, first : first + width], in_=result)
 
-        def rope_step(third, m):
+        def multiply(acc, m, product):
             shape = [P, 2, BANK_HEADS, PAIRS, 2]
+            nc.vector.tensor_tensor(
+                out=product.rearrange("p x (h i z) -> p x h i z", h=BANK_HEADS, z=2),
+                in0=acc[:].rearrange("p (x h i) -> p x h i", x=2, h=BANK_HEADS).unsqueeze(4).to_broadcast(shape),
+                in1=rope[:, m, :, :, :].unsqueeze(2).to_broadcast(shape),
+                op=ALU.mult,
+            )
+
+        def finish_half(third, m, half, acc, adder):
+            product = products.tile([P, 2, C], F32, name="product")
+            multiply(acc, m, product[:, :, 0:BANK])
+            result = rope_results.tile([P, C], F32, name="rope_result")
+            adder(out=result[:, 0:BANK], in0=product[:, 0, 0:BANK], in1=product[:, 1, 0:BANK], op=ALU.add)
+            store(third, m, half * BANK, BANK, result[:, 0:BANK])
+
+        def rope_half_step(third, m, half):
+            finish_half(third, m, half, project(psum_rope, third, m, half), nc.gpsimd.tensor_tensor)
+
+        def finish_four(third, m, accs):
             product = products.tile([P, 2, C], F32, name="product")
             for half in range(HALVES):
-                acc = project(psum_rope, third, m, half)
-                nc.vector.tensor_tensor(
-                    out=product[:, :, half * BANK : (half + 1) * BANK].rearrange(
-                        "p x (h i z) -> p x h i z", h=BANK_HEADS, z=2
-                    ),
-                    in0=acc[:].rearrange("p (h i x) -> p x h i", h=BANK_HEADS, x=2).unsqueeze(4).to_broadcast(shape),
-                    in1=rope[:, m, :, :, :].unsqueeze(2).to_broadcast(shape),
-                    op=ALU.mult,
-                )
+                multiply(accs[half], m, product[:, :, half * BANK : (half + 1) * BANK])
             result = rope_results.tile([P, C], F32, name="rope_result")
             nc.gpsimd.tensor_tensor(out=result[:], in0=product[:, 0, :], in1=product[:, 1, :], op=ALU.add)
-            store(third, m, result)
+            store(third, m, 0, C, result[:])
 
         def plain_step(third, m):
             result = plain_results.tile([P, C], F32, name="plain_result")
             for half in range(HALVES):
                 acc = project(psum_plain, third, m, half)
                 nc.scalar.copy(out=result[:, half * BANK : (half + 1) * BANK], in_=acc[:])
-            store(third, m, result)
+            store(third, m, 0, C, result[:])
 
-        X_PAIRS = TILES // 2
-        transpose_x_pair(0)
-        quantise_x_pair(0)
-        for piece in pieces_of(Q):
-            regroup_w(piece, on_vector=(piece[2] == 0))
-        take_sines()
-        for piece in pieces_of(Q):
-            quantise_w(piece)
+        vector_copy = nc.vector.tensor_copy
+        scalar_copy = nc.scalar.copy
+
+        HEAD_TILES = 4
+        finish_phase(0, HEAD_TILES)
+        finish_phase(HEAD_TILES, TILES)
+        transpose_x(0)
+        take_sines(0, HEAD_TILES)
+        transpose_x(1)
+        regroup_w((Q, 0, 0), vector_copy)
+        quantise_x(0, 1)
+        regroup_w((Q, 1, 0), vector_copy)
+        quantise_w((Q, 0, 0))
+        quantise_w((Q, 1, 0))
+        rope_half_step(Q, 0, 0)
+        transpose_x(2)
+        transpose_x(3)
+        quantise_x(1, 2)
+        rope_half_step(Q, 1, 0)
+        load_w(V, 0, 0, C)
+        load_w(V, 1, 0, C)
+        regroup_w((Q, 0, 1), scalar_copy)
+        quantise_x(2, 4)
+        rope_half_step(Q, 2, 0)
+        regroup_w((Q, 1, 1), scalar_copy)
+        rope_half_step(Q, 3, 0)
+        load_w(K, 0, 0, C)
+        load_w(K, 1, 0, C)
+        quantise_w((Q, 0, 1))
+        quantise_w((Q, 1, 1))
+        for m in range(HEAD_TILES, 8):
+            transpose_x(m)
+        take_sines(HEAD_TILES, 8)
+        for m in range(HEAD_TILES):
+            if m == 3:
+                quantise_x(4, 8)
+            rope_half_step(Q, m, 1)
+            transpose_x(8 + m)
+        take_sines(8, TILES)
+
+        def pieces_of(third):
+            return [(third, g, half) for half in range(HALVES) for g in range(PASSES)]
 
         later_pieces = pieces_of(V) + pieces_of(K)
-        rope_steps = [(third, m) for third in (Q, K) for m in range(TILES)]
-        FIRST_PIECE_STEP = 3
-        assert FIRST_PIECE_STEP + len(later_pieces) < TILES
-        FIRST_PLAIN_STEP = FIRST_PIECE_STEP + len(pieces_of(V)) + 1
+        rope_steps = [(Q, m) for m in range(HEAD_TILES, TILES)] + [(K, m) for m in range(TILES)]
+        FIRST_PLAIN_STEP = 6
+
+        def project_step(step):
+            third, m = rope_steps[step]
+            return [project(psum_rope, third, m, half) for half in range(HALVES)]
+
+        accs = project_step(0)
+        regroup_w(later_pieces[0], scalar_copy)
         for step, (third, m) in enumerate(rope_steps):
-            if 1 <= step < X_PAIRS:
-                quantise_x_pair(step)
-            rope_step(third, m)
-            if step + 1 < X_PAIRS:
-                transpose_x_pair(step + 1)
-            if 0 <= step - FIRST_PIECE_STEP < len(later_pieces):
-                regroup_w(later_pieces[step - FIRST_PIECE_STEP], on_vector=False)
-            if 0 <= step - FIRST_PIECE_STEP - 1 < len(later_pieces):
-                quantise_w(later_pieces[step - FIRST_PIECE_STEP - 1])
+            if step == 2:
+                quantise_x(8, 12)
+            if step == len(rope_steps) - 1:
+                finish_half(third, m, 0, accs[0], nc.gpsimd.tensor_tensor)
+                finish_half(third, m, 1, accs[1], nc.vector.tensor_tensor)
+            else:
+                finish_four(third, m, accs)
+            if step < len(later_pieces):
+                quantise_w(later_pieces[step])
+            if step + 1 < len(rope_steps):
+                accs = project_step(step + 1)
+            if step + 1 < len(later_pieces):
+                regroup_w(later_pieces[step + 1], scalar_copy)
             if 0 <= step - FIRST_PLAIN_STEP < TILES:
                 plain_step(V, step - FIRST_PLAIN_STEP)

@@ -43,8 +43,10 @@ def tile_memoryselfattention_pa_kernel(tc, x, short_term_memory, w_attn, out_0, 
 
     with ExitStack() as ctx:
         keep = ctx.enter_context(tc.tile_pool(name="keep", bufs=1))
+        x_load = ctx.enter_context(tc.tile_pool(name="x_load", bufs=3))
+        x_stage = ctx.enter_context(tc.tile_pool(name="x_stage", bufs=2))
         w_load = ctx.enter_context(tc.tile_pool(name="w_load", bufs=4))
-        w_stage = ctx.enter_context(tc.tile_pool(name="w_stage", bufs=4))
+        w_stage = ctx.enter_context(tc.tile_pool(name="w_stage", bufs=3))
         products = ctx.enter_context(tc.tile_pool(name="products", bufs=4))
         rope_results = ctx.enter_context(tc.tile_pool(name="rope_results", bufs=6))
         plain_results = ctx.enter_context(tc.tile_pool(name="plain_results", bufs=3))
@@ -53,54 +55,73 @@ def tile_memoryselfattention_pa_kernel(tc, x, short_term_memory, w_attn, out_0, 
         psum_plain = ctx.enter_context(tc.psum_pool(name="psum_plain", bufs=2))
         ctx.enter_context(tc.manual_schedule())
 
-        x_raw = keep.tile([P, TILES, C], BF16)
+        QUAD = 4
+        x_raw = {}
         w_raw = {}
 
         def load_x(first, count):
+            quad = first // QUAD
+            if quad not in x_raw:
+                x_raw[quad] = x_load.tile([P, QUAD, C], BF16, name="x_raw")
             if first < MEMORY_TILES:
                 rows = memory_rows[first * P : (first + count) * P, :]
             else:
                 rows = x_rows[(first - MEMORY_TILES) * P : (first - MEMORY_TILES + count) * P, :]
+            start = first % QUAD
             nc.sync.dma_start(
-                out=x_raw[:, first : first + count, :], in_=rows.rearrange("(m p) c -> p m c", p=P)
+                out=x_raw[quad][:, start : start + count, :], in_=rows.rearrange("(m p) c -> p m c", p=P)
             )
 
-        def load_w(third, g, first, width):
-            if (third, g) not in w_raw:
-                w_raw[third, g] = w_load.tile([P, PACK, C], BF16, name="w_raw")
+        def q_rows(g, half):
+            return w_raw[Q, g][:, half * PACK * BANK : (half + 1) * PACK * BANK].rearrange("p (t c) -> p t c", t=PACK)
+
+        def w_rows(third, g):
+            return w_raw[third, g][:].rearrange("p (t c) -> p t c", t=PACK)
+
+        def load_w(rows, third, g, first, width):
             columns = slice(third * C + first, third * C + first + width)
             nc.sync.dma_start(
-                out=w_raw[third, g][:, :, first : first + width],
-                in_=w_attn[K_PASS * g : K_PASS * (g + 1), columns].rearrange("(p t) c -> p t c", t=PACK),
+                out=rows, in_=w_attn[K_PASS * g : K_PASS * (g + 1), columns].rearrange("(p t) c -> p t c", t=PACK)
             )
 
+        def load_q(half):
+            for g in range(PASSES):
+                if half == 0:
+                    w_raw[Q, g] = w_load.tile([P, PACK * C], BF16, name="w_raw")
+                load_w(q_rows(g, half), Q, g, half * BANK, BANK)
+
+        def load_third(third):
+            for g in range(PASSES):
+                w_raw[third, g] = w_load.tile([P, PACK * C], BF16, name="w_raw")
+                load_w(w_rows(third, g), third, g, 0, C)
+
         load_x(0, 1)
-        load_w(Q, 0, 0, BANK)
-        load_w(Q, 1, 0, BANK)
+        load_q(0)
         load_x(1, 1)
         load_x(2, 2)
-        load_w(Q, 0, BANK, BANK)
-        load_w(Q, 1, BANK, BANK)
+        load_q(1)
         load_x(4, 4)
         load_x(8, 4)
 
-        warm = keep.tile([P, 1], F32)
-        nc.vector.memset(warm[:], 0.0)
+        one = keep.tile([P, 1], F32)
+        nc.vector.memset(one[:], 1.0)
         warm_out = keep.tile([P, 1], F32)
-        nc.scalar.activation(out=warm_out[:], in_=warm[:], func=ACT.Sin)
+        nc.scalar.activation(out=warm_out[:], in_=one[:], func=ACT.Sin)
 
-        position_int = keep.tile([P, TILES], I32)
-        nc.gpsimd.iota(position_int[:], pattern=[[P, TILES]], base=0, channel_multiplier=1)
+        position = keep.tile([P, TILES], F32)
+        nc.gpsimd.iota(
+            position[:], pattern=[[P, TILES]], base=0, channel_multiplier=1, allow_small_or_imprecise_dtypes=True
+        )
         identity = keep.tile([P, P], F32)
         make_identity(nc, identity[:])
 
-        one = keep.tile([P, 1], F32)
-        nc.vector.memset(one[:], 1.0)
+        SEEDS = 8
         turns_per_step = keep.tile([P, PAIRS], F32)
-        nc.vector.tensor_scalar_mul(out=turns_per_step[:, 0:1], in0=one[:], scalar1=1.0 / TWO_PI)
-        position = keep.tile([P, TILES], F32)
-        nc.vector.tensor_copy(out=position[:], in_=position_int[:])
-        width = 1
+        for i in range(SEEDS):
+            nc.vector.tensor_scalar_mul(
+                out=turns_per_step[:, i : i + 1], in0=one[:], scalar1=THETA ** (-i / PAIRS) / TWO_PI
+            )
+        width = SEEDS
         while width < PAIRS:
             nc.vector.tensor_scalar_mul(
                 out=turns_per_step[:, width : 2 * width],
@@ -109,32 +130,45 @@ def tile_memoryselfattention_pa_kernel(tc, x, short_term_memory, w_attn, out_0, 
             )
             width *= 2
 
-        phase = keep.tile([P, 3, TILES, PAIRS], F32)
+        phase = keep.tile([P, TILES, 3, PAIRS], F32)
         turns = keep.tile([P, TILES, PAIRS], F32)
-        nc.vector.tensor_tensor(
-            out=turns[:],
-            in0=position[:].unsqueeze(2).to_broadcast([P, TILES, PAIRS]),
-            in1=turns_per_step[:].unsqueeze(1).to_broadcast([P, TILES, PAIRS]),
-            op=ALU.mult,
-        )
         scratch = keep.tile([P, TILES, PAIRS], F32)
-        nc.vector.tensor_scalar_add(out=scratch[:], in0=turns[:], scalar1=ROUND_MAGIC)
-        nc.vector.scalar_tensor_tensor(
-            out=phase[:, 0, :, :], in0=scratch[:], scalar=ROUND_MAGIC, in1=turns[:], op0=ALU.subtract, op1=ALU.subtract
-        )
-
-
-        nc.vector.scalar_tensor_tensor(
-            out=scratch[:], in0=phase[:, 0, :, :], scalar=-1.0, in1=phase[:, 0, :, :], op0=ALU.mult, op1=ALU.max
-        )
-
-        def finish_phase(first, last):
-            some = slice(first, last)
+        HEAD_TILES = QUAD
+        parts = (slice(0, HEAD_TILES), slice(HEAD_TILES, TILES))
+        for part in parts:
+            shape = [P, part.stop - part.start, PAIRS]
+            nc.vector.tensor_tensor(
+                out=turns[:, part, :],
+                in0=position[:, part].unsqueeze(2).to_broadcast(shape),
+                in1=turns_per_step[:].unsqueeze(1).to_broadcast(shape),
+                op=ALU.mult,
+            )
+        for part in parts:
+            nc.vector.tensor_scalar_add(out=scratch[:, part, :], in0=turns[:, part, :], scalar1=ROUND_MAGIC)
+        for part in parts:
+            nc.vector.scalar_tensor_tensor(
+                out=phase[:, part, 0, :],
+                in0=scratch[:, part, :],
+                scalar=ROUND_MAGIC,
+                in1=turns[:, part, :],
+                op0=ALU.subtract,
+                op1=ALU.subtract,
+            )
+        for part in parts:
+            nc.vector.scalar_tensor_tensor(
+                out=scratch[:, part, :],
+                in0=phase[:, part, 0, :],
+                scalar=-1.0,
+                in1=phase[:, part, 0, :],
+                op0=ALU.mult,
+                op1=ALU.max,
+            )
+        for part in parts:
             nc.gpsimd.tensor_scalar(
-                out=phase[:, 2, some, :], in0=phase[:, 0, some, :], scalar1=-1.0, scalar2=0.0, op0=ALU.mult, op1=ALU.add
+                out=phase[:, part, 2, :], in0=phase[:, part, 0, :], scalar1=-1.0, scalar2=0.0, op0=ALU.mult, op1=ALU.add
             )
             nc.gpsimd.tensor_scalar(
-                out=phase[:, 1, some, :], in0=scratch[:, some, :], scalar1=-1.0, scalar2=0.25, op0=ALU.mult, op1=ALU.add
+                out=phase[:, part, 1, :], in0=scratch[:, part, :], scalar1=-1.0, scalar2=0.25, op0=ALU.mult, op1=ALU.add
             )
 
         rope = keep.tile([P, TILES, 2, PAIRS, 2], F32)
@@ -143,190 +177,200 @@ def tile_memoryselfattention_pa_kernel(tc, x, short_term_memory, w_attn, out_0, 
             for member in range(2):
                 nc.scalar.activation(
                     out=rope[:, first:last, member, :, :],
-                    in_=phase[:, member : member + 2, first:last, :].rearrange("p z m i -> p m i z"),
+                    in_=phase[:, first:last, member : member + 2, :].rearrange("p m z i -> p m i z"),
                     func=ACT.Sin,
                     scale=TWO_PI,
                 )
 
         TILE_WORDS = PASSES * P
-        x_grouped = keep.tile([P, TILES * TILE_WORDS * PACK], BF16, align_bytes=64)
         x_codes = keep.tile([P, TILES * TILE_WORDS], U32, align_bytes=64)
         x_scales = keep.tile([P, TILES * TILE_WORDS], U8, align_bytes=64)
+        x_grouped = {}
 
         def transpose_x(m):
-            x_words = x_raw[:, m, :].bitcast(F32)
-            flipped = psum_x.tile([P, PASSES * 2, P], F32, name="flipped")
+            quad, place = divmod(m, QUAD)
+            if quad not in x_grouped:
+                x_grouped[quad] = x_stage.tile([P, QUAD * TILE_WORDS * PACK], BF16, align_bytes=64, name="x_grouped")
+            x_words = x_raw[quad][:, place, :].bitcast(F32)
+            flipped = psum_x.tile([P, PASSES * 2, P], F32, name="bank")
             for j in range(PASSES * 2):
                 first = (j // 2) * 2 * P + j % 2
                 nc.tensor.transpose(flipped[:, j, :], x_words[:, first : first + 2 * P - 1 : 2], identity[:])
-            values = slice(m * TILE_WORDS * PACK, (m + 1) * TILE_WORDS * PACK)
+            values = slice(place * TILE_WORDS * PACK, (place + 1) * TILE_WORDS * PACK)
             nc.scalar.copy(
-                out=x_grouped[:, values].bitcast(F32).rearrange("p (g r u) -> p g r u", g=PASSES, u=2),
+                out=x_grouped[quad][:, values].bitcast(F32).rearrange("p (g r u) -> p g r u", g=PASSES, u=2),
                 in_=flipped[:].rearrange("p (g u) r -> p g r u", g=PASSES),
             )
 
         def quantise_x(first, last):
             words = slice(first * TILE_WORDS, last * TILE_WORDS)
+            start = first % QUAD * TILE_WORDS * PACK
             nc.vector.quantize_mx(
                 out=x_codes[:, words].bitcast(FP8X4),
                 scales=x_scales[:, words],
-                in_=x_grouped[:, first * TILE_WORDS * PACK : last * TILE_WORDS * PACK],
+                in_=x_grouped[first // QUAD][:, start : start + (last - first) * TILE_WORDS * PACK],
             )
 
-        w_codes = keep.tile([P, 3 * PASSES * C], U32, align_bytes=64)
-        w_scales = keep.tile([P, 3 * PASSES * C], U8, align_bytes=64)
+        w_codes = keep.tile([P, 3 * HALVES * PASSES * BANK], U32, align_bytes=64)
+        w_scales = keep.tile([P, 3 * HALVES * PASSES * BANK], U8, align_bytes=64)
         w_grouped = {}
 
-        def w_words(third, g, half):
-            start = (third * PASSES + g) * C + half * BANK
+        def w_words(third, half, g):
+            start = ((third * HALVES + half) * PASSES + g) * BANK
             return slice(start, start + BANK)
 
-        def regroup_w(piece, engine_copy):
-            third, g, half = piece
-            grouped = w_stage.tile([P, BANK, PACK], BF16, align_bytes=64, name="w_grouped")
-            w_grouped[piece] = grouped
-            rows = w_raw[third, g][:, :, half * BANK : (half + 1) * BANK]
+        def regroup_w(third, half, g, engine_copy):
+            if (third, half) not in w_grouped:
+                w_grouped[third, half] = w_stage.tile([P, PASSES, BANK, PACK], BF16, align_bytes=64, name="w_grouped")
+            grouped = w_grouped[third, half][:, g, :, :]
+            rows = q_rows(g, half) if third == Q else w_rows(third, g)[:, :, half * BANK : (half + 1) * BANK]
             if third == V:
                 engine_copy(
-                    out=grouped[:].rearrange("p (c i) t -> p c t i", i=4),
-                    in_=rows.rearrange("p t (c i) -> p c t i", i=4),
+                    out=grouped.rearrange("p (c i) t -> p c t i", i=4), in_=rows.rearrange("p t (c i) -> p c t i", i=4)
                 )
             else:
-                for x in range(2):
+                for member in range(2):
                     engine_copy(
-                        out=grouped[:, x * BANK // 2 : (x + 1) * BANK // 2, :].rearrange("p (c i) t -> p c t i", i=4),
-                        in_=rows.rearrange("p t (c i x) -> p x c t i", i=4, x=2)[:, 1 - x],
+                        out=grouped[:, member * BANK // 2 : (member + 1) * BANK // 2, :].rearrange(
+                            "p (c i) t -> p c t i", i=4
+                        ),
+                        in_=rows.rearrange("p t (c i x) -> p x c t i", i=4, x=2)[:, 1 - member],
                     )
 
-        def quantise_w(piece):
-            words = w_words(*piece)
+        def quantise_w(third, half, first=0, last=PASSES):
+            words = slice(w_words(third, half, first).start, w_words(third, half, last - 1).stop)
             nc.vector.quantize_mx(
                 out=w_codes[:, words].bitcast(FP8X4),
                 scales=w_scales[:, words],
-                in_=w_grouped[piece][:].rearrange("p c t -> p (c t)"),
-            )
-
-        def multiply_mx(acc, m, g, words, start, stop):
-            tokens = slice(m * TILE_WORDS + g * P, m * TILE_WORDS + (g + 1) * P)
-            nc.tensor.matmul_mx(
-                out=acc,
-                lhsT=x_codes[:, tokens].bitcast(FP8X4),
-                lhsT_scale=x_scales[:, tokens],
-                rhs=w_codes[:, words].bitcast(FP8X4),
-                rhs_scale=w_scales[:, words],
-                start=start,
-                stop=stop,
+                in_=w_grouped[third, half][:, first:last, :, :].rearrange("p g c t -> p (g c t)"),
             )
 
         def project(pool, third, m, half):
             acc = pool.tile([P, BANK], F32, name="acc")
             for g in range(PASSES):
-                multiply_mx(acc[:], m, g, w_words(third, g, half), g == 0, g == PASSES - 1)
+                tokens = slice(m * TILE_WORDS + g * P, m * TILE_WORDS + (g + 1) * P)
+                words = w_words(third, half, g)
+                nc.tensor.matmul_mx(
+                    out=acc[:],
+                    lhsT=x_codes[:, tokens].bitcast(FP8X4),
+                    lhsT_scale=x_scales[:, tokens],
+                    rhs=w_codes[:, words].bitcast(FP8X4),
+                    rhs_scale=w_scales[:, words],
+                    start=(g == 0),
+                    stop=(g == PASSES - 1),
+                )
             return acc
 
         def store(third, m, first, width, result):
             nc.sync.dma_start(out=outs[third][m * P : (m + 1) * P, first : first + width], in_=result)
 
-        def multiply(acc, m, product):
+        def multiply(engine_multiply, bank, m, product):
             shape = [P, 2, BANK_HEADS, PAIRS, 2]
-            nc.vector.tensor_tensor(
+            engine_multiply(
                 out=product.rearrange("p x (h i z) -> p x h i z", h=BANK_HEADS, z=2),
-                in0=acc[:].rearrange("p (x h i) -> p x h i", x=2, h=BANK_HEADS).unsqueeze(4).to_broadcast(shape),
+                in0=bank.rearrange("p (x h i) -> p x h i", x=2, h=BANK_HEADS).unsqueeze(4).to_broadcast(shape),
                 in1=rope[:, m, :, :, :].unsqueeze(2).to_broadcast(shape),
                 op=ALU.mult,
             )
 
-        def finish_half(third, m, half, acc, adder):
+        vector_tensors = nc.vector.tensor_tensor
+        gpsimd_tensors = nc.gpsimd.tensor_tensor
+
+        def finish_half(third, m, half, acc, engine_add):
             product = products.tile([P, 2, C], F32, name="product")
-            multiply(acc, m, product[:, :, 0:BANK])
+            multiply(vector_tensors, acc[:], m, product[:, :, 0:BANK])
             result = rope_results.tile([P, C], F32, name="rope_result")
-            adder(out=result[:, 0:BANK], in0=product[:, 0, 0:BANK], in1=product[:, 1, 0:BANK], op=ALU.add)
+            engine_add(out=result[:, 0:BANK], in0=product[:, 0, 0:BANK], in1=product[:, 1, 0:BANK], op=ALU.add)
             store(third, m, half * BANK, BANK, result[:, 0:BANK])
 
         def rope_half_step(third, m, half):
-            finish_half(third, m, half, project(psum_rope, third, m, half), nc.gpsimd.tensor_tensor)
+            finish_half(third, m, half, project(psum_rope, third, m, half), gpsimd_tensors)
 
-        def finish_four(third, m, accs):
+        def half_columns(half):
+            return slice(half * BANK, (half + 1) * BANK)
+
+        def multiply_step(m, accs):
             product = products.tile([P, 2, C], F32, name="product")
             for half in range(HALVES):
-                multiply(accs[half], m, product[:, :, half * BANK : (half + 1) * BANK])
+                multiply(vector_tensors, accs[half][:], m, product[:, :, half_columns(half)])
+            return product
+
+        def add_step(third, m, product):
             result = rope_results.tile([P, C], F32, name="rope_result")
-            nc.gpsimd.tensor_tensor(out=result[:], in0=product[:, 0, :], in1=product[:, 1, :], op=ALU.add)
+            gpsimd_tensors(out=result[:], in0=product[:, 0, :], in1=product[:, 1, :], op=ALU.add)
             store(third, m, 0, C, result[:])
 
-        def plain_step(third, m):
-            result = plain_results.tile([P, C], F32, name="plain_result")
-            for half in range(HALVES):
-                acc = project(psum_plain, third, m, half)
-                nc.scalar.copy(out=result[:, half * BANK : (half + 1) * BANK], in_=acc[:])
-            store(third, m, 0, C, result[:])
+        def plain_half(m, half, result):
+            acc = project(psum_plain, V, m, half)
+            nc.scalar.copy(out=result[:, half_columns(half)], in_=acc[:])
 
         vector_copy = nc.vector.tensor_copy
         scalar_copy = nc.scalar.copy
 
-        HEAD_TILES = 4
-        finish_phase(0, HEAD_TILES)
-        finish_phase(HEAD_TILES, TILES)
         transpose_x(0)
-        take_sines(0, HEAD_TILES)
         transpose_x(1)
-        regroup_w((Q, 0, 0), vector_copy)
-        quantise_x(0, 1)
-        regroup_w((Q, 1, 0), vector_copy)
-        quantise_w((Q, 0, 0))
-        quantise_w((Q, 1, 0))
-        rope_half_step(Q, 0, 0)
+        take_sines(0, HEAD_TILES)
         transpose_x(2)
         transpose_x(3)
+        regroup_w(Q, 0, 0, vector_copy)
+        quantise_x(0, 1)
+        regroup_w(Q, 0, 1, vector_copy)
+        quantise_w(Q, 0, 0, 1)
         quantise_x(1, 2)
-        rope_half_step(Q, 1, 0)
-        load_w(V, 0, 0, C)
-        load_w(V, 1, 0, C)
-        regroup_w((Q, 0, 1), scalar_copy)
+        quantise_w(Q, 0, 1, 2)
+        regroup_w(Q, 1, 0, scalar_copy)
+        rope_half_step(Q, 0, 0)
         quantise_x(2, 4)
+        rope_half_step(Q, 1, 0)
+        load_third(V)
+        regroup_w(Q, 1, 1, scalar_copy)
         rope_half_step(Q, 2, 0)
-        regroup_w((Q, 1, 1), scalar_copy)
-        rope_half_step(Q, 3, 0)
-        load_w(K, 0, 0, C)
-        load_w(K, 1, 0, C)
-        quantise_w((Q, 0, 1))
-        quantise_w((Q, 1, 1))
-        for m in range(HEAD_TILES, 8):
+        accs = [project(psum_rope, Q, 3, 0)]
+        for m in range(HEAD_TILES, 2 * QUAD):
             transpose_x(m)
-        take_sines(HEAD_TILES, 8)
-        for m in range(HEAD_TILES):
-            if m == 3:
-                quantise_x(4, 8)
-            rope_half_step(Q, m, 1)
-            transpose_x(8 + m)
-        take_sines(8, TILES)
+        quantise_w(Q, 1)
+        accs.append(project(psum_rope, Q, 0, 1))
+        finish_half(Q, 3, 0, accs[0], gpsimd_tensors)
+        load_third(K)
+        take_sines(HEAD_TILES, 2 * QUAD)
+        finish_half(Q, 0, 1, accs[1], gpsimd_tensors)
+        transpose_x(8)
+        transpose_x(9)
+        rope_half_step(Q, 1, 1)
+        transpose_x(10)
+        transpose_x(11)
+        rope_half_step(Q, 2, 1)
+        quantise_x(QUAD, 2 * QUAD)
+        rope_half_step(Q, 3, 1)
+        take_sines(2 * QUAD, TILES)
 
-        def pieces_of(third):
-            return [(third, g, half) for half in range(HALVES) for g in range(PASSES)]
-
-        later_pieces = pieces_of(V) + pieces_of(K)
+        later_pieces = [(third, half, g) for third in (V, K) for half in range(HALVES) for g in range(PASSES)]
         rope_steps = [(Q, m) for m in range(HEAD_TILES, TILES)] + [(K, m) for m in range(TILES)]
-        FIRST_PLAIN_STEP = 6
+        FIRST_PLAIN_STEP = 5
 
         def project_step(step):
             third, m = rope_steps[step]
             return [project(psum_rope, third, m, half) for half in range(HALVES)]
 
         accs = project_step(0)
-        regroup_w(later_pieces[0], scalar_copy)
+        regroup_w(*later_pieces[0], scalar_copy)
         for step, (third, m) in enumerate(rope_steps):
-            if step == 2:
-                quantise_x(8, 12)
             if step == len(rope_steps) - 1:
-                finish_half(third, m, 0, accs[0], nc.gpsimd.tensor_tensor)
-                finish_half(third, m, 1, accs[1], nc.vector.tensor_tensor)
+                finish_half(third, m, 0, accs[0], vector_tensors)
+                finish_half(third, m, 1, accs[1], vector_tensors)
             else:
-                finish_four(third, m, accs)
-            if step < len(later_pieces):
-                quantise_w(later_pieces[step])
+                add_step(third, m, multiply_step(m, accs))
+            if step == 2:
+                quantise_x(2 * QUAD, TILES)
+            if step < len(later_pieces) and step % 2 == 1:
+                third, half, g = later_pieces[step]
+                quantise_w(third, half)
             if step + 1 < len(rope_steps):
                 accs = project_step(step + 1)
             if step + 1 < len(later_pieces):
-                regroup_w(later_pieces[step + 1], scalar_copy)
+                regroup_w(*later_pieces[step + 1], scalar_copy)
             if 0 <= step - FIRST_PLAIN_STEP < TILES:
-                plain_step(V, step - FIRST_PLAIN_STEP)
+                result = plain_results.tile([P, C], F32, name="plain_result")
+                for half in range(HALVES):
+                    plain_half(step - FIRST_PLAIN_STEP, half, result)
+                store(V, step - FIRST_PLAIN_STEP, 0, C, result[:])

@@ -177,7 +177,7 @@ def tile_memoryselfattention_pa_kernel(tc, x, short_term_memory, w_attn, out_0, 
             for member in range(2):
                 nc.scalar.activation(
                     out=rope[:, first:last, member, :, :],
-                    in_=phase[:, first:last, member : member + 2, :].rearrange("p m z i -> p m i z"),
+                    in_=phase[:, first:last, 1 - member : 3 - member, :].rearrange("p m z i -> p m i z"),
                     func=ACT.Sin,
                     scale=TWO_PI,
                 )
@@ -224,18 +224,9 @@ def tile_memoryselfattention_pa_kernel(tc, x, short_term_memory, w_attn, out_0, 
                 w_grouped[third, half] = w_stage.tile([P, PASSES, BANK, PACK], BF16, align_bytes=64, name="w_grouped")
             grouped = w_grouped[third, half][:, g, :, :]
             rows = q_rows(g, half) if third == Q else w_rows(third, g)[:, :, half * BANK : (half + 1) * BANK]
-            if third == V:
-                engine_copy(
-                    out=grouped.rearrange("p (c i) t -> p c t i", i=4), in_=rows.rearrange("p t (c i) -> p c t i", i=4)
-                )
-            else:
-                for member in range(2):
-                    engine_copy(
-                        out=grouped[:, member * BANK // 2 : (member + 1) * BANK // 2, :].rearrange(
-                            "p (c i) t -> p c t i", i=4
-                        ),
-                        in_=rows.rearrange("p t (c i x) -> p x c t i", i=4, x=2)[:, 1 - member],
-                    )
+            engine_copy(
+                out=grouped.rearrange("p (c i) t -> p c t i", i=4), in_=rows.rearrange("p t (c i) -> p c t i", i=4)
+            )
 
         def quantise_w(third, half, first=0, last=PASSES):
             words = slice(w_words(third, half, first).start, w_words(third, half, last - 1).stop)
@@ -268,7 +259,7 @@ def tile_memoryselfattention_pa_kernel(tc, x, short_term_memory, w_attn, out_0, 
             shape = [P, 2, BANK_HEADS, PAIRS, 2]
             engine_multiply(
                 out=product.rearrange("p x (h i z) -> p x h i z", h=BANK_HEADS, z=2),
-                in0=bank.rearrange("p (x h i) -> p x h i", x=2, h=BANK_HEADS).unsqueeze(4).to_broadcast(shape),
+                in0=bank.rearrange("p (h i x) -> p x h i", h=BANK_HEADS, x=2).unsqueeze(4).to_broadcast(shape),
                 in1=rope[:, m, :, :, :].unsqueeze(2).to_broadcast(shape),
                 op=ALU.mult,
             )

@@ -72,8 +72,8 @@ def tile_memoryselfattention_pa_kernel(tc, x, short_term_memory, w_attn, out_0, 
                 out=x_raw[quad][:, start : start + count, :], in_=rows.rearrange("(m p) c -> p m c", p=P)
             )
 
-        def q_rows(g, half):
-            return w_raw[Q, g][:, half * PACK * BANK : (half + 1) * PACK * BANK].rearrange("p (t c) -> p t c", t=PACK)
+        def q_rows(g, first, last):
+            return w_raw[Q, g][:, PACK * first : PACK * last].rearrange("p (t c) -> p t c", t=PACK)
 
         def w_rows(third, g):
             return w_raw[third, g][:].rearrange("p (t c) -> p t c", t=PACK)
@@ -84,22 +84,24 @@ def tile_memoryselfattention_pa_kernel(tc, x, short_term_memory, w_attn, out_0, 
                 out=rows, in_=w_attn[K_PASS * g : K_PASS * (g + 1), columns].rearrange("(p t) c -> p t c", t=PACK)
             )
 
-        def load_q(half):
+        def load_q(first, last):
             for g in range(PASSES):
-                if half == 0:
+                if first == 0:
                     w_raw[Q, g] = w_load.tile([P, PACK * C], BF16, name="w_raw")
-                load_w(q_rows(g, half), Q, g, half * BANK, BANK)
+                load_w(q_rows(g, first, last), Q, g, first, last - first)
 
         def load_third(third):
             for g in range(PASSES):
                 w_raw[third, g] = w_load.tile([P, PACK * C], BF16, name="w_raw")
                 load_w(w_rows(third, g), third, g, 0, C)
 
+        QUARTER = BANK // 2
         load_x(0, 1)
-        load_q(0)
+        load_q(0, QUARTER)
         load_x(1, 1)
+        load_q(QUARTER, BANK)
         load_x(2, 2)
-        load_q(1)
+        load_q(BANK, C)
         load_x(4, 4)
         load_x(8, 4)
 
@@ -134,8 +136,9 @@ def tile_memoryselfattention_pa_kernel(tc, x, short_term_memory, w_attn, out_0, 
         turns = keep.tile([P, TILES, PAIRS], F32)
         scratch = keep.tile([P, TILES, PAIRS], F32)
         HEAD_TILES = QUAD
-        parts = (slice(0, HEAD_TILES), slice(HEAD_TILES, TILES))
-        for part in parts:
+        early, late = slice(0, HEAD_TILES), slice(HEAD_TILES, TILES)
+
+        def phase_turns(part):
             shape = [P, part.stop - part.start, PAIRS]
             nc.vector.tensor_tensor(
                 out=turns[:, part, :],
@@ -143,9 +146,11 @@ def tile_memoryselfattention_pa_kernel(tc, x, short_term_memory, w_attn, out_0, 
                 in1=turns_per_step[:].unsqueeze(1).to_broadcast(shape),
                 op=ALU.mult,
             )
-        for part in parts:
+
+        def phase_round(part):
             nc.vector.tensor_scalar_add(out=scratch[:, part, :], in0=turns[:, part, :], scalar1=ROUND_MAGIC)
-        for part in parts:
+
+        def phase_difference(part):
             nc.vector.scalar_tensor_tensor(
                 out=phase[:, part, 0, :],
                 in0=scratch[:, part, :],
@@ -154,7 +159,8 @@ def tile_memoryselfattention_pa_kernel(tc, x, short_term_memory, w_attn, out_0, 
                 op0=ALU.subtract,
                 op1=ALU.subtract,
             )
-        for part in parts:
+
+        def phase_distance(part):
             nc.vector.scalar_tensor_tensor(
                 out=scratch[:, part, :],
                 in0=phase[:, part, 0, :],
@@ -163,11 +169,12 @@ def tile_memoryselfattention_pa_kernel(tc, x, short_term_memory, w_attn, out_0, 
                 op0=ALU.mult,
                 op1=ALU.max,
             )
-        for part in parts:
-            nc.gpsimd.tensor_scalar(
+
+        def phase_planes(part, engine):
+            engine.tensor_scalar(
                 out=phase[:, part, 2, :], in0=phase[:, part, 0, :], scalar1=-1.0, scalar2=0.0, op0=ALU.mult, op1=ALU.add
             )
-            nc.gpsimd.tensor_scalar(
+            engine.tensor_scalar(
                 out=phase[:, part, 1, :], in0=scratch[:, part, :], scalar1=-1.0, scalar2=0.25, op0=ALU.mult, op1=ALU.add
             )
 
@@ -219,13 +226,36 @@ def tile_memoryselfattention_pa_kernel(tc, x, short_term_memory, w_attn, out_0, 
             start = ((third * HALVES + half) * PASSES + g) * BANK
             return slice(start, start + BANK)
 
+        def regroup_columns(grouped, rows, engine_copy):
+            engine_copy(
+                out=grouped.rearrange("p (c i) t -> p c t i", i=4), in_=rows.rearrange("p t (c i) -> p c t i", i=4)
+            )
+
         def regroup_w(third, half, g, engine_copy):
             if (third, half) not in w_grouped:
                 w_grouped[third, half] = w_stage.tile([P, PASSES, BANK, PACK], BF16, align_bytes=64, name="w_grouped")
-            grouped = w_grouped[third, half][:, g, :, :]
-            rows = q_rows(g, half) if third == Q else w_rows(third, g)[:, :, half * BANK : (half + 1) * BANK]
-            engine_copy(
-                out=grouped.rearrange("p (c i) t -> p c t i", i=4), in_=rows.rearrange("p t (c i) -> p c t i", i=4)
+            first, last = half * BANK, (half + 1) * BANK
+            rows = q_rows(g, first, last) if third == Q else w_rows(third, g)[:, :, first:last]
+            regroup_columns(w_grouped[third, half][:, g, :, :], rows, engine_copy)
+
+        quarter_grouped = {}
+
+        def regroup_quarter(quarter, g, engine_copy):
+            if quarter not in quarter_grouped:
+                quarter_grouped[quarter] = w_stage.tile(
+                    [P, PASSES, QUARTER, PACK], BF16, align_bytes=64, name="w_grouped"
+                )
+            regroup_columns(
+                quarter_grouped[quarter][:, g, :, :], q_rows(g, quarter * QUARTER, (quarter + 1) * QUARTER), engine_copy
+            )
+
+        def quantise_quarter(quarter, g):
+            start = w_words(Q, 0, g).start + quarter * QUARTER
+            words = slice(start, start + QUARTER)
+            nc.vector.quantize_mx(
+                out=w_codes[:, words].bitcast(FP8X4),
+                scales=w_scales[:, words],
+                in_=quarter_grouped[quarter][:, g, :, :].rearrange("p c t -> p (c t)"),
             )
 
         def quantise_w(third, half, first=0, last=PASSES):
@@ -236,13 +266,14 @@ def tile_memoryselfattention_pa_kernel(tc, x, short_term_memory, w_attn, out_0, 
                 in_=w_grouped[third, half][:, first:last, :, :].rearrange("p g c t -> p (g c t)"),
             )
 
-        def project(pool, third, m, half):
+        def project(pool, third, m, half, first=0, last=BANK):
             acc = pool.tile([P, BANK], F32, name="acc")
             for g in range(PASSES):
                 tokens = slice(m * TILE_WORDS + g * P, m * TILE_WORDS + (g + 1) * P)
-                words = w_words(third, half, g)
+                start = w_words(third, half, g).start
+                words = slice(start + first, start + last)
                 nc.tensor.matmul_mx(
-                    out=acc[:],
+                    out=acc[:, 0 : last - first],
                     lhsT=x_codes[:, tokens].bitcast(FP8X4),
                     lhsT_scale=x_scales[:, tokens],
                     rhs=w_codes[:, words].bitcast(FP8X4),
@@ -255,11 +286,12 @@ def tile_memoryselfattention_pa_kernel(tc, x, short_term_memory, w_attn, out_0, 
         def store(third, m, first, width, result):
             nc.sync.dma_start(out=outs[third][m * P : (m + 1) * P, first : first + width], in_=result)
 
-        def multiply(engine_multiply, bank, m, product):
-            shape = [P, 2, BANK_HEADS, PAIRS, 2]
-            engine_multiply(
-                out=product.rearrange("p x (h i z) -> p x h i z", h=BANK_HEADS, z=2),
-                in0=bank.rearrange("p (h i x) -> p x h i", h=BANK_HEADS, x=2).unsqueeze(4).to_broadcast(shape),
+        def multiply(bank, m, product):
+            heads = bank.shape[1] // HEAD
+            shape = [P, 2, heads, PAIRS, 2]
+            nc.vector.tensor_tensor(
+                out=product.rearrange("p x (h i z) -> p x h i z", h=heads, z=2),
+                in0=bank.rearrange("p (h i x) -> p x h i", h=heads, x=2).unsqueeze(4).to_broadcast(shape),
                 in1=rope[:, m, :, :, :].unsqueeze(2).to_broadcast(shape),
                 op=ALU.mult,
             )
@@ -267,15 +299,20 @@ def tile_memoryselfattention_pa_kernel(tc, x, short_term_memory, w_attn, out_0, 
         vector_tensors = nc.vector.tensor_tensor
         gpsimd_tensors = nc.gpsimd.tensor_tensor
 
-        def finish_half(third, m, half, acc, engine_add):
+        def finish_columns(third, m, first, width, acc, engine_add):
             product = products.tile([P, 2, C], F32, name="product")
-            multiply(vector_tensors, acc[:], m, product[:, :, 0:BANK])
+            multiply(acc[:, 0:width], m, product[:, :, 0:width])
             result = rope_results.tile([P, C], F32, name="rope_result")
-            engine_add(out=result[:, 0:BANK], in0=product[:, 0, 0:BANK], in1=product[:, 1, 0:BANK], op=ALU.add)
-            store(third, m, half * BANK, BANK, result[:, 0:BANK])
+            engine_add(out=result[:, 0:width], in0=product[:, 0, 0:width], in1=product[:, 1, 0:width], op=ALU.add)
+            store(third, m, first, width, result[:, 0:width])
+
+        def rope_quarter_step(m, quarter):
+            first = quarter * QUARTER
+            acc = project(psum_rope, Q, m, 0, first, first + QUARTER)
+            finish_columns(Q, m, first, QUARTER, acc, gpsimd_tensors)
 
         def rope_half_step(third, m, half):
-            finish_half(third, m, half, project(psum_rope, third, m, half), gpsimd_tensors)
+            finish_columns(third, m, half * BANK, BANK, project(psum_rope, third, m, half), gpsimd_tensors)
 
         def half_columns(half):
             return slice(half * BANK, (half + 1) * BANK)
@@ -283,13 +320,26 @@ def tile_memoryselfattention_pa_kernel(tc, x, short_term_memory, w_attn, out_0, 
         def multiply_step(m, accs):
             product = products.tile([P, 2, C], F32, name="product")
             for half in range(HALVES):
-                multiply(vector_tensors, accs[half][:], m, product[:, :, half_columns(half)])
+                multiply(accs[half][:], m, product[:, :, half_columns(half)])
             return product
 
         def add_step(third, m, product):
             result = rope_results.tile([P, C], F32, name="rope_result")
             gpsimd_tensors(out=result[:], in0=product[:, 0, :], in1=product[:, 1, :], op=ALU.add)
             store(third, m, 0, C, result[:])
+
+        def tensor_add_half(third, m, half, product, result):
+            total = psum_x.tile([P, BANK], F32, name="bank")
+            for member in range(2):
+                nc.tensor.matmul(
+                    total[:],
+                    lhsT=identity[:],
+                    rhs=product[:, member, half_columns(half)],
+                    start=(member == 0),
+                    stop=(member == 1),
+                )
+            nc.scalar.copy(out=result[:, half_columns(half)], in_=total[:])
+            store(third, m, half * BANK, BANK, result[:, half_columns(half)])
 
         def plain_half(m, half, result):
             acc = project(psum_plain, V, m, half)
@@ -298,46 +348,65 @@ def tile_memoryselfattention_pa_kernel(tc, x, short_term_memory, w_attn, out_0, 
         vector_copy = nc.vector.tensor_copy
         scalar_copy = nc.scalar.copy
 
+        phase_turns(early)
+        phase_turns(late)
+        phase_round(early)
+        phase_round(late)
+        phase_difference(early)
+        phase_distance(early)
+        phase_planes(early, nc.vector)
         transpose_x(0)
-        transpose_x(1)
         take_sines(0, HEAD_TILES)
+        transpose_x(1)
+        regroup_quarter(0, 0, vector_copy)
+        regroup_quarter(0, 1, vector_copy)
+        quantise_x(0, 1)
+        quantise_quarter(0, 0)
+        quantise_quarter(0, 1)
+        regroup_quarter(1, 0, vector_copy)
+        regroup_quarter(1, 1, scalar_copy)
+        regroup_w(Q, 1, 0, scalar_copy)
+        quantise_x(1, 2)
+        rope_quarter_step(0, 0)
+        quantise_quarter(1, 0)
+        rope_quarter_step(1, 0)
+        quantise_quarter(1, 1)
+        phase_difference(late)
+        phase_distance(late)
+        phase_planes(late, nc.gpsimd)
         transpose_x(2)
         transpose_x(3)
-        regroup_w(Q, 0, 0, vector_copy)
-        quantise_x(0, 1)
-        regroup_w(Q, 0, 1, vector_copy)
-        quantise_w(Q, 0, 0, 1)
-        quantise_x(1, 2)
-        quantise_w(Q, 0, 1, 2)
-        regroup_w(Q, 1, 0, scalar_copy)
-        rope_half_step(Q, 0, 0)
-        quantise_x(2, 4)
-        rope_half_step(Q, 1, 0)
-        load_third(V)
+        rope_quarter_step(0, 1)
         regroup_w(Q, 1, 1, scalar_copy)
+        quantise_x(2, 4)
+        rope_quarter_step(1, 1)
+        load_third(V)
+        transpose_x(4)
+        transpose_x(5)
         rope_half_step(Q, 2, 0)
         accs = [project(psum_rope, Q, 3, 0)]
-        for m in range(HEAD_TILES, 2 * QUAD):
-            transpose_x(m)
+        transpose_x(6)
+        transpose_x(7)
         quantise_w(Q, 1)
         accs.append(project(psum_rope, Q, 0, 1))
-        finish_half(Q, 3, 0, accs[0], gpsimd_tensors)
+        finish_columns(Q, 3, 0, BANK, accs[0], gpsimd_tensors)
         load_third(K)
+        finish_columns(Q, 0, BANK, BANK, accs[1], gpsimd_tensors)
         take_sines(HEAD_TILES, 2 * QUAD)
-        finish_half(Q, 0, 1, accs[1], gpsimd_tensors)
+        rope_half_step(Q, 1, 1)
         transpose_x(8)
         transpose_x(9)
-        rope_half_step(Q, 1, 1)
+        quantise_x(QUAD, 2 * QUAD)
+        rope_half_step(Q, 2, 1)
         transpose_x(10)
         transpose_x(11)
-        rope_half_step(Q, 2, 1)
-        quantise_x(QUAD, 2 * QUAD)
         rope_half_step(Q, 3, 1)
         take_sines(2 * QUAD, TILES)
 
         later_pieces = [(third, half, g) for third in (V, K) for half in range(HALVES) for g in range(PASSES)]
         rope_steps = [(Q, m) for m in range(HEAD_TILES, TILES)] + [(K, m) for m in range(TILES)]
         FIRST_PLAIN_STEP = 5
+        TENSOR_STEPS = (0, 3,)
 
         def project_step(step):
             third, m = rope_steps[step]
@@ -345,17 +414,25 @@ def tile_memoryselfattention_pa_kernel(tc, x, short_term_memory, w_attn, out_0, 
 
         accs = project_step(0)
         regroup_w(*later_pieces[0], scalar_copy)
+        waiting = []
         for step, (third, m) in enumerate(rope_steps):
             if step == len(rope_steps) - 1:
-                finish_half(third, m, 0, accs[0], vector_tensors)
-                finish_half(third, m, 1, accs[1], vector_tensors)
+                finish_columns(third, m, 0, BANK, accs[0], vector_tensors)
+                finish_columns(third, m, BANK, BANK, accs[1], vector_tensors)
+            elif step == len(rope_steps) - 2:
+                finish_columns(third, m, 0, BANK, accs[0], gpsimd_tensors)
+                product = products.tile([P, 2, C], F32, name="product")
+                multiply(accs[1][:], m, product[:, :, half_columns(1)])
+                result = rope_results.tile([P, C], F32, name="rope_result")
+                waiting.append((third, m, 1, product, result))
             else:
-                add_step(third, m, multiply_step(m, accs))
+                product = multiply_step(m, accs)
+                if step not in TENSOR_STEPS:
+                    add_step(third, m, product)
             if step == 2:
                 quantise_x(2 * QUAD, TILES)
             if step < len(later_pieces) and step % 2 == 1:
-                third, half, g = later_pieces[step]
-                quantise_w(third, half)
+                quantise_w(*later_pieces[step][:2])
             if step + 1 < len(rope_steps):
                 accs = project_step(step + 1)
             if step + 1 < len(later_pieces):
@@ -365,3 +442,8 @@ def tile_memoryselfattention_pa_kernel(tc, x, short_term_memory, w_attn, out_0, 
                 for half in range(HALVES):
                     plain_half(step - FIRST_PLAIN_STEP, half, result)
                 store(V, step - FIRST_PLAIN_STEP, 0, C, result[:])
+            if waiting:
+                tensor_add_half(*waiting.pop(0))
+            if step in TENSOR_STEPS:
+                result = rope_results.tile([P, C], F32, name="rope_result")
+                waiting.extend((third, m, half, product, result) for half in range(HALVES))

@@ -84,8 +84,8 @@ def tile_memoryselfattention_pa_kernel(tc, x, short_term_memory, w_attn, out_0, 
                 out=rows, in_=w_attn[K_PASS * g : K_PASS * (g + 1), columns].rearrange("(p t) c -> p t c", t=PACK)
             )
 
-        def load_q(first, last):
-            for g in range(PASSES):
+        def load_q(first, last, only=None):
+            for g in range(PASSES) if only is None else (only,):
                 if first == 0:
                     w_raw[Q, g] = w_load.tile([P, PACK * C], BF16, name="w_raw")
                 load_w(q_rows(g, first, last), Q, g, first, last - first)
@@ -100,8 +100,9 @@ def tile_memoryselfattention_pa_kernel(tc, x, short_term_memory, w_attn, out_0, 
         load_q(0, QUARTER)
         load_x(1, 1)
         load_q(QUARTER, BANK)
+        load_q(BANK, C, 0)
         load_x(2, 2)
-        load_q(BANK, C)
+        load_q(BANK, C, 1)
         load_x(4, 4)
         load_x(8, 4)
 
@@ -146,6 +147,12 @@ def tile_memoryselfattention_pa_kernel(tc, x, short_term_memory, w_attn, out_0, 
                 in1=turns_per_step[:].unsqueeze(1).to_broadcast(shape),
                 op=ALU.mult,
             )
+
+        def phase_turns_by_scalar(part):
+            for m in range(part.start, part.stop):
+                nc.scalar.activation(
+                    out=turns[:, m, :], in_=turns_per_step[:], func=ACT.Copy, scale=position[:, m : m + 1]
+                )
 
         def phase_round(part):
             nc.vector.tensor_scalar_add(out=scratch[:, part, :], in0=turns[:, part, :], scalar1=ROUND_MAGIC)
@@ -299,12 +306,17 @@ def tile_memoryselfattention_pa_kernel(tc, x, short_term_memory, w_attn, out_0, 
         vector_tensors = nc.vector.tensor_tensor
         gpsimd_tensors = nc.gpsimd.tensor_tensor
 
+        def add_columns(engine_add, third, m, first, width, product, start=None):
+            start = first if start is None else start
+            result = rope_results.tile([P, C], F32, name="rope_result")
+            some = slice(start, start + width)
+            engine_add(out=result[:, 0:width], in0=product[:, 0, some], in1=product[:, 1, some], op=ALU.add)
+            store(third, m, first, width, result[:, 0:width])
+
         def finish_columns(third, m, first, width, acc, engine_add):
             product = products.tile([P, 2, C], F32, name="product")
             multiply(acc[:, 0:width], m, product[:, :, 0:width])
-            result = rope_results.tile([P, C], F32, name="rope_result")
-            engine_add(out=result[:, 0:width], in0=product[:, 0, 0:width], in1=product[:, 1, 0:width], op=ALU.add)
-            store(third, m, first, width, result[:, 0:width])
+            add_columns(engine_add, third, m, first, width, product, 0)
 
         def rope_quarter_step(m, quarter):
             first = quarter * QUARTER
@@ -317,18 +329,7 @@ def tile_memoryselfattention_pa_kernel(tc, x, short_term_memory, w_attn, out_0, 
         def half_columns(half):
             return slice(half * BANK, (half + 1) * BANK)
 
-        def multiply_step(m, accs):
-            product = products.tile([P, 2, C], F32, name="product")
-            for half in range(HALVES):
-                multiply(accs[half][:], m, product[:, :, half_columns(half)])
-            return product
-
-        def add_step(third, m, product):
-            result = rope_results.tile([P, C], F32, name="rope_result")
-            gpsimd_tensors(out=result[:], in0=product[:, 0, :], in1=product[:, 1, :], op=ALU.add)
-            store(third, m, 0, C, result[:])
-
-        def tensor_add_half(third, m, half, product, result):
+        def tensor_add_half(third, m, half, product):
             total = psum_x.tile([P, BANK], F32, name="bank")
             for member in range(2):
                 nc.tensor.matmul(
@@ -338,8 +339,9 @@ def tile_memoryselfattention_pa_kernel(tc, x, short_term_memory, w_attn, out_0, 
                     start=(member == 0),
                     stop=(member == 1),
                 )
-            nc.scalar.copy(out=result[:, half_columns(half)], in_=total[:])
-            store(third, m, half * BANK, BANK, result[:, half_columns(half)])
+            result = rope_results.tile([P, C], F32, name="rope_result")
+            nc.scalar.copy(out=result[:, 0:BANK], in_=total[:])
+            store(third, m, half * BANK, BANK, result[:, 0:BANK])
 
         def plain_half(m, half, result):
             acc = project(psum_plain, V, m, half)
@@ -349,9 +351,8 @@ def tile_memoryselfattention_pa_kernel(tc, x, short_term_memory, w_attn, out_0, 
         scalar_copy = nc.scalar.copy
 
         phase_turns(early)
-        phase_turns(late)
+        phase_turns_by_scalar(late)
         phase_round(early)
-        phase_round(late)
         phase_difference(early)
         phase_distance(early)
         phase_planes(early, nc.vector)
@@ -363,7 +364,7 @@ def tile_memoryselfattention_pa_kernel(tc, x, short_term_memory, w_attn, out_0, 
         quantise_x(0, 1)
         quantise_quarter(0, 0)
         quantise_quarter(0, 1)
-        regroup_quarter(1, 0, vector_copy)
+        regroup_quarter(1, 0, scalar_copy)
         regroup_quarter(1, 1, scalar_copy)
         regroup_w(Q, 1, 0, scalar_copy)
         quantise_x(1, 2)
@@ -371,6 +372,7 @@ def tile_memoryselfattention_pa_kernel(tc, x, short_term_memory, w_attn, out_0, 
         quantise_quarter(1, 0)
         rope_quarter_step(1, 0)
         quantise_quarter(1, 1)
+        phase_round(late)
         phase_difference(late)
         phase_distance(late)
         phase_planes(late, nc.gpsimd)
@@ -405,8 +407,9 @@ def tile_memoryselfattention_pa_kernel(tc, x, short_term_memory, w_attn, out_0, 
 
         later_pieces = [(third, half, g) for third in (V, K) for half in range(HALVES) for g in range(PASSES)]
         rope_steps = [(Q, m) for m in range(HEAD_TILES, TILES)] + [(K, m) for m in range(TILES)]
-        FIRST_PLAIN_STEP = 5
-        TENSOR_STEPS = (0, 3,)
+        FIRST_PLAIN_STEP = 4
+        BY_GPSIMD, BY_TENSOR, BY_VECTOR = range(3)
+        ADDERS = {0: (BY_TENSOR, BY_TENSOR), 3: (BY_TENSOR, BY_TENSOR), 16: (BY_GPSIMD, BY_TENSOR), 17: (BY_GPSIMD, BY_TENSOR), 18: (BY_VECTOR, BY_GPSIMD), 19: (BY_VECTOR, BY_VECTOR)}
 
         def project_step(step):
             third, m = rope_steps[step]
@@ -416,19 +419,17 @@ def tile_memoryselfattention_pa_kernel(tc, x, short_term_memory, w_attn, out_0, 
         regroup_w(*later_pieces[0], scalar_copy)
         waiting = []
         for step, (third, m) in enumerate(rope_steps):
-            if step == len(rope_steps) - 1:
-                finish_columns(third, m, 0, BANK, accs[0], vector_tensors)
-                finish_columns(third, m, BANK, BANK, accs[1], vector_tensors)
-            elif step == len(rope_steps) - 2:
-                finish_columns(third, m, 0, BANK, accs[0], gpsimd_tensors)
-                product = products.tile([P, 2, C], F32, name="product")
-                multiply(accs[1][:], m, product[:, :, half_columns(1)])
-                result = rope_results.tile([P, C], F32, name="rope_result")
-                waiting.append((third, m, 1, product, result))
+            product = products.tile([P, 2, C], F32, name="product")
+            for half in range(HALVES):
+                multiply(accs[half][:], m, product[:, :, half_columns(half)])
+            if step in ADDERS:
+                for half, adder in enumerate(ADDERS[step]):
+                    if adder != BY_TENSOR:
+                        add_columns(
+                            vector_tensors if adder == BY_VECTOR else gpsimd_tensors, third, m, half * BANK, BANK, product
+                        )
             else:
-                product = multiply_step(m, accs)
-                if step not in TENSOR_STEPS:
-                    add_step(third, m, product)
+                add_columns(gpsimd_tensors, third, m, 0, C, product)
             if step == 2:
                 quantise_x(2 * QUAD, TILES)
             if step < len(later_pieces) and step % 2 == 1:
@@ -437,13 +438,15 @@ def tile_memoryselfattention_pa_kernel(tc, x, short_term_memory, w_attn, out_0, 
                 accs = project_step(step + 1)
             if step + 1 < len(later_pieces):
                 regroup_w(*later_pieces[step + 1], scalar_copy)
-            if 0 <= step - FIRST_PLAIN_STEP < TILES:
-                result = plain_results.tile([P, C], F32, name="plain_result")
+            tile = step - FIRST_PLAIN_STEP
+            if 0 <= tile < TILES:
+                plain = plain_results.tile([P, C], F32, name="plain_result")
                 for half in range(HALVES):
-                    plain_half(step - FIRST_PLAIN_STEP, half, result)
-                store(V, step - FIRST_PLAIN_STEP, 0, C, result[:])
+                    plain_half(tile, half, plain)
+                store(V, tile, 0, C, plain[:])
             if waiting:
                 tensor_add_half(*waiting.pop(0))
-            if step in TENSOR_STEPS:
-                result = rope_results.tile([P, C], F32, name="rope_result")
-                waiting.extend((third, m, half, product, result) for half in range(HALVES))
+            if step in ADDERS:
+                waiting.extend((third, m, half, product) for half in range(HALVES) if ADDERS[step][half] == BY_TENSOR)
+        for half in waiting:
+            tensor_add_half(*half)

@@ -47,8 +47,7 @@ def tile_memoryselfattention_pa_kernel(tc, x, short_term_memory, w_attn, out_0, 
         x_stage = ctx.enter_context(tc.tile_pool(name="x_stage", bufs=2))
         w_load = ctx.enter_context(tc.tile_pool(name="w_load", bufs=4))
         w_stage = ctx.enter_context(tc.tile_pool(name="w_stage", bufs=3))
-        products = ctx.enter_context(tc.tile_pool(name="products", bufs=4))
-        rope_results = ctx.enter_context(tc.tile_pool(name="rope_results", bufs=6))
+        products = ctx.enter_context(tc.tile_pool(name="products", bufs=7))
         plain_results = ctx.enter_context(tc.tile_pool(name="plain_results", bufs=3))
         psum_x = ctx.enter_context(tc.psum_pool(name="psum_x", bufs=2))
         psum_rope = ctx.enter_context(tc.psum_pool(name="psum_rope", bufs=4))
@@ -308,10 +307,9 @@ def tile_memoryselfattention_pa_kernel(tc, x, short_term_memory, w_attn, out_0, 
 
         def add_columns(engine_add, third, m, first, width, product, start=None):
             start = first if start is None else start
-            result = rope_results.tile([P, C], F32, name="rope_result")
-            some = slice(start, start + width)
-            engine_add(out=result[:, 0:width], in0=product[:, 0, some], in1=product[:, 1, some], op=ALU.add)
-            store(third, m, first, width, result[:, 0:width])
+            result = product[:, 0, start : start + width]
+            engine_add(out=result, in0=result, in1=product[:, 1, start : start + width], op=ALU.add)
+            store(third, m, first, width, result)
 
         def finish_columns(third, m, first, width, acc, engine_add):
             product = products.tile([P, 2, C], F32, name="product")
@@ -339,9 +337,9 @@ def tile_memoryselfattention_pa_kernel(tc, x, short_term_memory, w_attn, out_0, 
                     start=(member == 0),
                     stop=(member == 1),
                 )
-            result = rope_results.tile([P, C], F32, name="rope_result")
-            nc.scalar.copy(out=result[:, 0:BANK], in_=total[:])
-            store(third, m, half * BANK, BANK, result[:, 0:BANK])
+            result = product[:, 0, half_columns(half)]
+            nc.scalar.copy(out=result, in_=total[:])
+            store(third, m, half * BANK, BANK, result)
 
         def plain_half(m, half, result):
             acc = project(psum_plain, V, m, half)

import math
from contextlib import ExitStack

import concourse.mybir as mybir
from concourse.masks import make_identity

F32 = mybir.dt.float32
BF16 = mybir.dt.bfloat16
I32 = mybir.dt.int32
U32 = mybir.dt.uint32
U8 = mybir.dt.uint8
FP8X4 = mybir.dt.float8_e4m3fn_x4
ALU = mybir.AluOpType
ACT = mybir.ActivationFunctionType

P = 128
PACK = 4
K_PASS = P * PACK
MEMORY_TOKENS = 512
TOKENS = 1536
C = 1024
PASSES = C // K_PASS
TILES = TOKENS // P
MEMORY_TILES = MEMORY_TOKENS // P
BANK = 512
HALVES = C // BANK
HEAD = 128
PAIRS = HEAD // 2
BANK_HEADS = BANK // HEAD
THETA = 10000.0
Q, K, V = 0, 1, 2
ROUND_MAGIC = 1.5 * 2.0**23

FLOPS = 2 * TOKENS * C * 3 * C
TWO_PI = 2.0 * math.pi


def tile_memoryselfattention_pa_kernel(tc, x, short_term_memory, w_attn, out_0, out_1, out_2):
    nc = tc.nc
    memory_rows = short_term_memory.flatten_outer_dims()
    x_rows = x.flatten_outer_dims()
    outs = [o.rearrange("b n h d -> (b n) (h d)") for o in (out_0, out_1, out_2)]

    with ExitStack() as ctx:
        keep = ctx.enter_context(tc.tile_pool(name="keep", bufs=1))
        x_load = ctx.enter_context(tc.tile_pool(name="x_load", bufs=3))
        x_stage = ctx.enter_context(tc.tile_pool(name="x_stage", bufs=2))
        w_load = ctx.enter_context(tc.tile_pool(name="w_load", bufs=4))
        w_stage = ctx.enter_context(tc.tile_pool(name="w_stage", bufs=3))
        products = ctx.enter_context(tc.tile_pool(name="products", bufs=7))
        plain_results = ctx.enter_context(tc.tile_pool(name="plain_results", bufs=3))
        psum_x = ctx.enter_context(tc.psum_pool(name="psum_x", bufs=2))
        psum_rope = ctx.enter_context(tc.psum_pool(name="psum_rope", bufs=4))
        psum_plain = ctx.enter_context(tc.psum_pool(name="psum_plain", bufs=2))
        ctx.enter_context(tc.manual_schedule())

        QUAD = 4
        x_raw = {}
        w_raw = {}

        def load_x(first, count):
            quad = first // QUAD
            if quad not in x_raw:
                x_raw[quad] = x_load.tile([P, QUAD, C], BF16, name="x_raw")
            if first < MEMORY_TILES:
                rows = memory_rows[first * P : (first + count) * P, :]
            else:
                rows = x_rows[(first - MEMORY_TILES) * P : (first - MEMORY_TILES + count) * P, :]
            start = first % QUAD
            nc.sync.dma_start(
                out=x_raw[quad][:, start : start + count, :], in_=rows.rearrange("(m p) c -> p m c", p=P)
            )

        def q_rows(g, first, last):
            return w_raw[Q, g][:, PACK * first : PACK * last].rearrange("p (t c) -> p t c", t=PACK)

        def w_rows(third, g):
            return w_raw[third, g][:].rearrange("p (t c) -> p t c", t=PACK)

        def load_w(rows, third, g, first, width):
            columns = slice(third * C + first, third * C + first + width)
            nc.sync.dma_start(
                out=rows, in_=w_attn[K_PASS * g : K_PASS * (g + 1), columns].rearrange("(p t) c -> p t c", t=PACK)
            )

        def load_q(first, last, only=None):
            for g in range(PASSES) if only is None else (only,):
                if first == 0:
                    w_raw[Q, g] = w_load.tile([P, PACK * C], BF16, name="w_raw")
                load_w(q_rows(g, first, last), Q, g, first, last - first)

        def load_third(third):
            for g in range(PASSES):
                w_raw[third, g] = w_load.tile([P, PACK * C], BF16, name="w_raw")
                load_w(w_rows(third, g), third, g, 0, C)

        QUARTER = BANK // 2
        load_x(0, 1)
        load_q(0, QUARTER)
        load_x(1, 1)
        load_q(QUARTER, BANK)
        load_q(BANK, C, 0)
        load_x(2, 2)
        load_q(BANK, C, 1)
        load_x(4, 4)
        load_x(8, 4)

        one = keep.tile([P, 1], F32)
        nc.vector.memset(one[:], 1.0)
        warm_out = keep.tile([P, 1], F32)
        nc.scalar.activation(out=warm_out[:], in_=one[:], func=ACT.Sin)

        position = keep.tile([P, TILES], F32)
        nc.gpsimd.iota(
            position[:], pattern=[[P, TILES]], base=0, channel_multiplier=1, allow_small_or_imprecise_dtypes=True
        )
        identity = keep.tile([P, P], F32)
        make_identity(nc, identity[:])

        SEEDS = 8
        turns_per_step = keep.tile([P, PAIRS], F32)
        for i in range(SEEDS):
            nc.vector.tensor_scalar_mul(
                out=turns_per_step[:, i : i + 1], in0=one[:], scalar1=THETA ** (-i / PAIRS) / TWO_PI
            )
        width = SEEDS
        while width < PAIRS:
            nc.vector.tensor_scalar_mul(
                out=turns_per_step[:, width : 2 * width],
                in0=turns_per_step[:, 0:width],
                scalar1=THETA ** (-width / PAIRS),
            )
            width *= 2

        phase = keep.tile([P, TILES, 3, PAIRS], F32)
        turns = keep.tile([P, TILES, PAIRS], F32)
        scratch = keep.tile([P, TILES, PAIRS], F32)
        HEAD_TILES = QUAD
        early, late = slice(0, HEAD_TILES), slice(HEAD_TILES, TILES)

        def phase_turns(part):
            shape = [P, part.stop - part.start, PAIRS]
            nc.vector.tensor_tensor(
                out=turns[:, part, :],
                in0=position[:, part].unsqueeze(2).to_broadcast(shape),
                in1=turns_per_step[:].unsqueeze(1).to_broadcast(shape),
                op=ALU.mult,
            )

        def phase_turns_by_scalar(part):
            for m in range(part.start, part.stop):
                nc.scalar.activation(
                    out=turns[:, m, :], in_=turns_per_step[:], func=ACT.Copy, scale=position[:, m : m + 1]
                )

        def phase_round(part):
            nc.vector.tensor_scalar_add(out=scratch[:, part, :], in0=turns[:, part, :], scalar1=ROUND_MAGIC)

        def phase_difference(part):
            nc.vector.scalar_tensor_tensor(
                out=phase[:, part, 0, :],
                in0=scratch[:, part, :],
                scalar=ROUND_MAGIC,
                in1=turns[:, part, :],
                op0=ALU.subtract,
                op1=ALU.subtract,
            )

        def phase_distance(part):
            nc.vector.scalar_tensor_tensor(
                out=scratch[:, part, :],
                in0=phase[:, part, 0, :],
                scalar=-1.0,
                in1=phase[:, part, 0, :],
                op0=ALU.mult,
                op1=ALU.max,
            )

        def phase_planes(part, engine):
            engine.tensor_scalar(
                out=phase[:, part, 2, :], in0=phase[:, part, 0, :], scalar1=-1.0, scalar2=0.0, op0=ALU.mult, op1=ALU.add
            )
            engine.tensor_scalar(
                out=phase[:, part, 1, :], in0=scratch[:, part, :], scalar1=-1.0, scalar2=0.25, op0=ALU.mult, op1=ALU.add
            )

        rope = keep.tile([P, TILES, 2, PAIRS, 2], F32)

        def take_sines(first, last):
            for member in range(2):
                nc.scalar.activation(
                    out=rope[:, first:last, member, :, :],
                    in_=phase[:, first:last, 1 - member : 3 - member, :].rearrange("p m z i -> p m i z"),
                    func=ACT.Sin,
                    scale=TWO_PI,
                )

        TILE_WORDS = PASSES * P
        x_codes = keep.tile([P, TILES * TILE_WORDS], U32, align_bytes=64)
        x_scales = keep.tile([P, TILES * TILE_WORDS], U8, align_bytes=64)
        x_grouped = {}

        def transpose_x(m):
            quad, place = divmod(m, QUAD)
            if quad not in x_grouped:
                x_grouped[quad] = x_stage.tile([P, QUAD * TILE_WORDS * PACK], BF16, align_bytes=64, name="x_grouped")
            x_words = x_raw[quad][:, place, :].bitcast(F32)
            flipped = psum_x.tile([P, PASSES * 2, P], F32, name="bank")
            for j in range(PASSES * 2):
                first = (j // 2) * 2 * P + j % 2
                nc.tensor.transpose(flipped[:, j, :], x_words[:, first : first + 2 * P - 1 : 2], identity[:])
            values = slice(place * TILE_WORDS * PACK, (place + 1) * TILE_WORDS * PACK)
            nc.scalar.copy(
                out=x_grouped[quad][:, values].bitcast(F32).rearrange("p (g r u) -> p g r u", g=PASSES, u=2),
                in_=flipped[:].rearrange("p (g u) r -> p g r u", g=PASSES),
            )

        def quantise_x(first, last):
            words = slice(first * TILE_WORDS, last * TILE_WORDS)
            start = first % QUAD * TILE_WORDS * PACK
            nc.vector.quantize_mx(
                out=x_codes[:, words].bitcast(FP8X4),
                scales=x_scales[:, words],
                in_=x_grouped[first // QUAD][:, start : start + (last - first) * TILE_WORDS * PACK],
            )

        w_codes = keep.tile([P, 3 * HALVES * PASSES * BANK], U32, align_bytes=64)
        w_scales = keep.tile([P, 3 * HALVES * PASSES * BANK], U8, align_bytes=64)
        w_grouped = {}

        def w_words(third, half, g):
            start = ((third * HALVES + half) * PASSES + g) * BANK
            return slice(start, start + BANK)

        def regroup_columns(grouped, rows, engine_copy):
            engine_copy(
                out=grouped.rearrange("p (c i) t -> p c t i", i=4), in_=rows.rearrange("p t (c i) -> p c t i", i=4)
            )

        def regroup_w(third, half, g, engine_copy):
            if (third, half) not in w_grouped:
                w_grouped[third, half] = w_stage.tile([P, PASSES, BANK, PACK], BF16, align_bytes=64, name="w_grouped")
            first, last = half * BANK, (half + 1) * BANK
            rows = q_rows(g, first, last) if third == Q else w_rows(third, g)[:, :, first:last]
            regroup_columns(w_grouped[third, half][:, g, :, :], rows, engine_copy)

        quarter_grouped = {}

        def regroup_quarter(quarter, g, engine_copy):
            if quarter not in quarter_grouped:
                quarter_grouped[quarter] = w_stage.tile(
                    [P, PASSES, QUARTER, PACK], BF16, align_bytes=64, name="w_grouped"
                )
            regroup_columns(
                quarter_grouped[quarter][:, g, :, :], q_rows(g, quarter * QUARTER, (quarter + 1) * QUARTER), engine_copy
            )

        def quantise_quarter(quarter, g):
            start = w_words(Q, 0, g).start + quarter * QUARTER
            words = slice(start, start + QUARTER)
            nc.vector.quantize_mx(
                out=w_codes[:, words].bitcast(FP8X4),
                scales=w_scales[:, words],
                in_=quarter_grouped[quarter][:, g, :, :].rearrange("p c t -> p (c t)"),
            )

        def quantise_w(third, half, first=0, last=PASSES):
            words = slice(w_words(third, half, first).start, w_words(third, half, last - 1).stop)
            nc.vector.quantize_mx(
                out=w_codes[:, words].bitcast(FP8X4),
                scales=w_scales[:, words],
                in_=w_grouped[third, half][:, first:last, :, :].rearrange("p g c t -> p (g c t)"),
            )

        def project(pool, third, m, half, first=0, last=BANK):
            acc = pool.tile([P, BANK], F32, name="acc")
            for g in range(PASSES):
                tokens = slice(m * TILE_WORDS + g * P, m * TILE_WORDS + (g + 1) * P)
                start = w_words(third, half, g).start
                words = slice(start + first, start + last)
                nc.tensor.matmul_mx(
                    out=acc[:, 0 : last - first],
                    lhsT=x_codes[:, tokens].bitcast(FP8X4),
                    lhsT_scale=x_scales[:, tokens],
                    rhs=w_codes[:, words].bitcast(FP8X4),
                    rhs_scale=w_scales[:, words],
                    start=(g == 0),
                    stop=(g == PASSES - 1),
                )
            return acc

        def store(third, m, first, width, result):
            nc.sync.dma_start(out=outs[third][m * P : (m + 1) * P, first : first + width], in_=result)

        def multiply(bank, m, product):
            heads = bank.shape[1] // HEAD
            shape = [P, 2, heads, PAIRS, 2]
            nc.vector.tensor_tensor(
                out=product.rearrange("p x (h i z) -> p x h i z", h=heads, z=2),
                in0=bank.rearrange("p (h i x) -> p x h i", h=heads, x=2).unsqueeze(4).to_broadcast(shape),
                in1=rope[:, m, :, :, :].unsqueeze(2).to_broadcast(shape),
                op=ALU.mult,
            )

        vector_tensors = nc.vector.tensor_tensor
        gpsimd_tensors = nc.gpsimd.tensor_tensor

        def add_columns(engine_add, third, m, first, width, product, start=None):
            start = first if start is None else start
            result = product[:, 0, start : start + width]
            engine_add(out=result, in0=result, in1=product[:, 1, start : start + width], op=ALU.add)
            store(third, m, first, width, result)

        def finish_columns(third, m, first, width, acc, engine_add):
            product = products.tile([P, 2, C], F32, name="product")
            multiply(acc[:, 0:width], m, product[:, :, 0:width])
            add_columns(engine_add, third, m, first, width, product, 0)

        def rope_quarter_step(m, quarter):
            first = quarter * QUARTER
            acc = project(psum_rope, Q, m, 0, first, first + QUARTER)
            finish_columns(Q, m, first, QUARTER, acc, gpsimd_tensors)

        def rope_half_step(third, m, half):
            finish_columns(third, m, half * BANK, BANK, project(psum_rope, third, m, half), gpsimd_tensors)

        def half_columns(half):
            return slice(half * BANK, (half + 1) * BANK)

        def tensor_add_half(third, m, half, product):
            total = psum_x.tile([P, BANK], F32, name="bank")
            for member in range(2):
                nc.tensor.matmul(
                    total[:],
                    lhsT=identity[:],
                    rhs=product[:, member, half_columns(half)],
                    start=(member == 0),
                    stop=(member == 1),
                )
            result = product[:, 0, half_columns(half)]
            nc.scalar.copy(out=result, in_=total[:])
            store(third, m, half * BANK, BANK, result)

        def plain_half(m, half, result):
            acc = project(psum_plain, V, m, half)
            nc.scalar.copy(out=result[:, half_columns(half)], in_=acc[:])

        vector_copy = nc.vector.tensor_copy
        scalar_copy = nc.scalar.copy

        phase_turns(early)
        phase_turns_by_scalar(late)
        phase_round(early)
        phase_difference(early)
        phase_distance(early)
        phase_planes(early, nc.vector)
        transpose_x(0)
        take_sines(0, HEAD_TILES)
        transpose_x(1)
        regroup_quarter(0, 0, vector_copy)
        regroup_quarter(0, 1, vector_copy)
        quantise_x(0, 1)
        quantise_quarter(0, 0)
        quantise_quarter(0, 1)
        regroup_quarter(1, 0, scalar_copy)
        regroup_quarter(1, 1, scalar_copy)
        regroup_w(Q, 1, 0, scalar_copy)
        quantise_x(1, 2)
        rope_quarter_step(0, 0)
        quantise_quarter(1, 0)
        rope_quarter_step(1, 0)
        quantise_quarter(1, 1)
        phase_round(late)
        phase_difference(late)
        phase_distance(late)
        phase_planes(late, nc.gpsimd)
        transpose_x(2)
        transpose_x(3)
        rope_quarter_step(0, 1)
        regroup_w(Q, 1, 1, scalar_copy)
        quantise_x(2, 4)
        rope_quarter_step(1, 1)
        load_third(V)
        transpose_x(4)
        transpose_x(5)
        rope_half_step(Q, 2, 0)
        accs = [project(psum_rope, Q, 3, 0)]
        transpose_x(6)
        transpose_x(7)
        quantise_w(Q, 1)
        accs.append(project(psum_rope, Q, 0, 1))
        finish_columns(Q, 3, 0, BANK, accs[0], gpsimd_tensors)
        load_third(K)
        finish_columns(Q, 0, BANK, BANK, accs[1], gpsimd_tensors)
        take_sines(HEAD_TILES, 2 * QUAD)
        rope_half_step(Q, 1, 1)
        transpose_x(8)
        transpose_x(9)
        quantise_x(QUAD, 2 * QUAD)
        rope_half_step(Q, 2, 1)
        transpose_x(10)
        transpose_x(11)
        rope_half_step(Q, 3, 1)
        take_sines(2 * QUAD, TILES)

        later_pieces = [(third, half, g) for third in (V, K) for half in range(HALVES) for g in range(PASSES)]
        rope_steps = [(Q, m) for m in range(HEAD_TILES, TILES)] + [(K, m) for m in range(TILES)]
        FIRST_PLAIN_STEP = 4
        BY_GPSIMD, BY_TENSOR, BY_VECTOR = range(3)
        ADDERS = {0: (BY_TENSOR, BY_TENSOR), 3: (BY_TENSOR, BY_TENSOR), 16: (BY_GPSIMD, BY_TENSOR), 17: (BY_GPSIMD, BY_TENSOR), 18: (BY_VECTOR, BY_GPSIMD), 19: (BY_VECTOR, BY_VECTOR)}

        def project_step(step):
            third, m = rope_steps[step]
            return [project(psum_rope, third, m, half) for half in range(HALVES)]

        accs = project_step(0)
        regroup_w(*later_pieces[0], scalar_copy)
        waiting = []
        for step, (third, m) in enumerate(rope_steps):
            product = products.tile([P, 2, C], F32, name="product")
            for half in range(HALVES):
                multiply(accs[half][:], m, product[:, :, half_columns(half)])
            if step in ADDERS:
                for half, adder in enumerate(ADDERS[step]):
                    if adder != BY_TENSOR:
                        add_columns(
                            vector_tensors if adder == BY_VECTOR else gpsimd_tensors, third, m, half * BANK, BANK, product
                        )
            else:
                add_columns(gpsimd_tensors, third, m, 0, C, product)
            if step == 2:
                quantise_x(2 * QUAD, TILES)
            if step < len(later_pieces) and step % 2 == 1:
                quantise_w(*later_pieces[step][:2])
            if step + 1 < len(rope_steps):
                accs = project_step(step + 1)
            if step + 1 < len(later_pieces):
                regroup_w(*later_pieces[step + 1], scalar_copy)
            tile = step - FIRST_PLAIN_STEP
            if 0 <= tile < TILES:
                plain = plain_results.tile([P, C], F32, name="plain_result")
                for half in range(HALVES):
                    plain_half(tile, half, plain)
                store(V, tile, 0, C, plain[:])
            if waiting:
                tensor_add_half(*waiting.pop(0))
            if step in ADDERS:
                waiting.extend((third, m, half, product) for half in range(HALVES) if ADDERS[step][half] == BY_TENSOR)
        for half in waiting:
            tensor_add_half(*half)
